import numpy as np
import ml_dtypes


def mxq(x, axis, fmt="e4m3"):
    dtype, down = {"e4m3": (ml_dtypes.float8_e4m3fn, 7), "e5m2": (ml_dtypes.float8_e5m2, 14)}[fmt]
    v = np.moveaxis(np.asarray(x, np.float32).astype(ml_dtypes.bfloat16).astype(np.float64), axis, -1)
    blocks = v.reshape(v.shape[:-1] + (-1, 32))
    amax = np.abs(blocks).max(-1, keepdims=True)
    byte = np.maximum(np.where(amax > 0, np.frexp(amax)[1] - 1 + 127, 0) - down, 1)
    scale = np.exp2(byte - 127.0)
    codes = (blocks / scale).astype(np.float32).astype(dtype).astype(np.float64)
    return np.moveaxis((codes * scale).reshape(v.shape), -1, axis)


WIDE = False


def mx_kscale(k):
    if not WIDE:
        return np.ones(k)
    levels = np.array([10, -10, 5, -5, 0])
    a = np.random.permutation(np.resize(levels, k // 512 * 4)).reshape(k // 512, 4)
    idx = np.arange(k)
    return np.exp2(a[idx // 512, idx % 128 // 32])


BF16 = ml_dtypes.bfloat16


def bf(x):
    return np.asarray(x, np.float32).astype(BF16)


def f64(x):
    return np.asarray(x).astype(np.float64)


E2M1 = np.array([0.0, 0.5, 1.0, 1.5, 2.0, 3.0, 4.0, 6.0, -0.0, -0.5, -1.0, -1.5, -2.0, -3.0, -4.0, -6.0])


def pack_weight(w, fmt):
    k, n = w.shape
    w = f64(bf(w)).reshape(k // 32, 32, n)
    amax = np.abs(w).max(1)
    if fmt == "e4m3":
        byte = np.frexp(amax)[1] - 1 + 127 - 7
    else:
        mant, ex = np.frexp(amax / 6.0)
        byte = np.where(mant > 0.5, ex, ex - 1) + 127
    byte = np.clip(np.where(amax > 0, byte, 1), 1, 254)
    scaled = (w * np.exp2(127.0 - byte)[:, None, :]).reshape(k, n).astype(np.float32)
    by_word = np.ascontiguousarray(scaled.reshape(k // 512, 128, 4, n).transpose(0, 1, 3, 2))
    if fmt == "e4m3":
        words = by_word.astype(ml_dtypes.float8_e4m3fn).view(np.uint8)
    else:
        c = by_word.astype(ml_dtypes.float4_e2m1fn).view(np.uint8) & 0xF
        words = c[..., 0::2] | (c[..., 1::2] << 4)
    return np.ascontiguousarray(words), np.ascontiguousarray(byte.astype(np.uint8).reshape(k // 512, 16, n))


def unpack_weight(words, scales, fmt):
    g, p, n, _ = words.shape
    if fmt == "e4m3":
        vals = np.ascontiguousarray(words).view(ml_dtypes.float8_e4m3fn).astype(np.float64)
    else:
        nib = np.empty((g, p, n, 4), np.uint8)
        nib[..., 0::2] = words & 0xF
        nib[..., 1::2] = words >> 4
        vals = E2M1[nib]
    vals = vals * np.repeat(np.exp2(scales.astype(np.float64) - 127.0), 8, axis=1)[..., None]
    return vals.transpose(0, 1, 3, 2).reshape(g * 512, n)


N, K, F, NB = 1024, 8192, 384, 32
EPS = 1e-6
FMT = "e4m3"


def erf(v):
    a = np.minimum(np.abs(v), 6.0)
    term = a.copy()
    total = a.copy()
    for n in range(1, 130):
        term = term * (2.0 * a * a / (2.0 * n + 1.0))
        total = total + term
    return np.sign(v) * (2.0 / np.sqrt(np.pi)) * np.exp(-a * a) * total


def gelu(v):
    return 0.5 * v * (1.0 + erf(v / np.sqrt(2.0)))


def setup_inputs():
    s = mx_kscale(K)
    edge = np.random.random_sample((N, N)) < NB / N
    x = bf(np.random.standard_normal((N, K)) * s)
    adj = bf(np.random.random_sample((N, N)) * edge)
    W1_words, W1_scales = pack_weight(np.random.standard_normal((K, F)) * 3.0 / np.sqrt(K) / s[:, None], FMT)
    return {"x": x,
            "adj": adj,
            "W1_words": W1_words,
            "W1_scales": W1_scales,
            "b1": bf(np.random.standard_normal(F) * 0.3),
            "ln_gamma": bf(1.0 + 0.1 * np.random.standard_normal(F)),
            "ln_beta": bf(0.1 * np.random.standard_normal(F))}


def reference(x, adj, W1_words, W1_scales, b1, ln_gamma, ln_beta):
    a = f64(adj)
    h = (mxq(f64(x), 1, "e4m3") @ unpack_weight(W1_words, W1_scales, FMT)) + f64(b1)
    deg = a.sum(axis=1) + 1.0
    dinv = np.where(deg > 0, deg ** -0.5, 0.0)
    hs = dinv[:, None] * h
    agg = (mxq(a, 1, "e4m3") @ mxq(hs, 0, "e4m3")) + hs
    g = gelu(dinv[:, None] * agg)
    mu = g.mean(axis=-1, keepdims=True)
    var = ((g - mu) ** 2).mean(axis=-1, keepdims=True)
    return (g - mu) / np.sqrt(var + EPS) * f64(ln_gamma) + f64(ln_beta)

@@ -1,0 +1,322 @@
+from contextlib import ExitStack
+
+import concourse.mybir as mybir
+from concourse.masks import make_identity
+
+F32 = mybir.dt.float32
+BF16 = mybir.dt.bfloat16
+I32 = mybir.dt.int32
+U32 = mybir.dt.uint32
+U8 = mybir.dt.uint8
+FP8X4 = mybir.dt.float8_e4m3fn_x4
+ACT = mybir.ActivationFunctionType
+ALU = mybir.AluOpType
+
+P = 128
+PACK = 4
+K_PASS = P * PACK
+NODES = 1024
+K = 8192
+FEAT = 384
+EPS = 1e-6
+
+TILES = NODES // P
+NODE_GROUPS = NODES // K_PASS
+TILES_PER_GROUP = TILES // NODE_GROUPS
+K_GROUPS = K // K_PASS
+HALF_GROUPS = K_GROUPS // 2
+HALF_K = HALF_GROUPS * K_PASS
+HALF_WORDS = HALF_K // 2
+HALVES = 2 * TILES
+BANK_GROUPS = 2
+WIDE = 256
+FEATURE_CUTS = ((0, WIDE), (WIDE, FEAT))
+
+FLOPS = 2 * NODES * K * FEAT + 2 * NODES * NODES * FEAT
+
+
+def tile_gcnlayer_pa_k_kernel(tc, x, adj, W1_words, W1_scales, b1, ln_gamma, ln_beta, out):
+    nc = tc.nc
+
+    def by_node_tile(dram):
+        return dram.rearrange("(n p e) w -> n e p w", n=TILES // 2, p=P, e=2)
+
+    x_tiles = by_node_tile(x)
+    adj_tiles = by_node_tile(adj)
+    out_tiles = by_node_tile(out)
+
+    with ExitStack() as ctx:
+        ctx.enter_context(tc.manual_schedule())
+        keep = ctx.enter_context(tc.tile_pool(name="keep", bufs=1))
+        raw_pool = ctx.enter_context(tc.tile_pool(name="raw", bufs=3))
+        sorted_pool = ctx.enter_context(tc.tile_pool(name="sorted", bufs=4))
+        grouped_pool = ctx.enter_context(tc.tile_pool(name="grouped", bufs=3))
+        codes_pool = ctx.enter_context(tc.tile_pool(name="codes", bufs=3))
+        adj_pool = ctx.enter_context(tc.tile_pool(name="adj", bufs=2))
+        tail_pool = ctx.enter_context(tc.tile_pool(name="tail", bufs=3))
+        banks = ctx.enter_context(tc.psum_pool(name="banks", bufs=6))
+        h_banks = ctx.enter_context(tc.psum_pool(name="h_banks", bufs=2))
+
+        identity = keep.tile([P, P], F32)
+        ones = keep.tile([P, P], BF16)
+        rows = keep.tile([P, 3, 512], BF16)
+        spread = keep.tile([P, 3, FEAT], F32)
+        minus_half = keep.tile([P, 1], F32)
+        warm = keep.tile([P, 1], F32)
+        w_codes = keep.tile([P, K_GROUPS, FEAT], U32, align_bytes=64)
+        w_scales = keep.tile([P, K_GROUPS, FEAT], U8, align_bytes=64)
+        adj_codes = keep.tile([P, TILES, NODE_GROUPS, P], U32, align_bytes=64)
+        adj_scales = keep.tile([P, TILES, NODE_GROUPS, P], U8, align_bytes=64)
+        hb = keep.tile([P, TILES, FEAT], F32)
+        hs_grouped = keep.tile([P, NODE_GROUPS, FEAT, PACK], BF16, align_bytes=64)
+        hs_codes = keep.tile([P, NODE_GROUPS, FEAT], U32, align_bytes=64)
+        hs_scales = keep.tile([P, NODE_GROUPS, FEAT], U8, align_bytes=64)
+        deg = keep.tile([P, TILES], F32)
+        deg1 = keep.tile([P, TILES], F32)
+        dinv = keep.tile([P, TILES], F32)
+        g_sum = keep.tile([P, TILES], F32)
+        minus_mean = keep.tile([P, TILES], F32)
+        sq_sum = keep.tile([P, TILES], F32)
+        var_eps = keep.tile([P, TILES], F32)
+        rstd = keep.tile([P, TILES], F32)
+
+        raw = {}
+        ordered = {}
+        grouped = {}
+        x_codes = {}
+        x_scales = {}
+        adj_raw = {}
+        adj_grouped = {}
+        h_acc = {}
+
+        def load_x(q):
+            n, h = divmod(q, 2)
+            raw[q] = raw_pool.tile([P, HALF_K], BF16, name="raw")
+            nc.sync.dma_start(out=raw[q][:], in_=x_tiles[n // 2, n % 2, :, h * HALF_K : (h + 1) * HALF_K])
+
+        def load_adj(n):
+            adj_raw[n] = adj_pool.tile([P, NODES], BF16, name="adj_raw")
+            nc.sync.dma_start(out=adj_raw[n][:], in_=adj_tiles[n // 2, n % 2, :, :])
+
+        def sort_words(q):
+            ordered[q] = sorted_pool.tile([P, HALF_K], BF16, name="ordered")
+            nc.vector.tensor_copy(
+                out=ordered[q][:].bitcast(F32).rearrange("n (g u p) -> n g u p", g=HALF_GROUPS, u=2),
+                in_=raw[q][:].bitcast(F32).rearrange("n (g p u) -> n g u p", g=HALF_GROUPS, u=2),
+            )
+
+        def transpose_x(q):
+            words = ordered[q][:].bitcast(F32).rearrange("n (g u p) -> n g u p", g=HALF_GROUPS, u=2)
+            grouped[q] = grouped_pool.tile([P, HALF_K], BF16, name="grouped", align_bytes=64)
+            pairs = grouped[q][:].bitcast(F32).rearrange("p (g n u) -> p g n u", g=HALF_GROUPS, u=2)
+            for g0 in range(0, HALF_GROUPS, BANK_GROUPS):
+                bank = banks.tile([P, BANK_GROUPS, 2, P], F32, name="bank")
+                for g in range(BANK_GROUPS):
+                    for u in range(2):
+                        nc.tensor.transpose(bank[:, g, u, :], words[:, g0 + g, u, :], identity[:])
+                nc.scalar.copy(
+                    out=pairs[:, g0 : g0 + BANK_GROUPS, :, :],
+                    in_=bank[:].rearrange("p g u n -> p g n u"),
+                )
+
+        def quantise_x(q):
+            n, h = divmod(q, 2)
+            if h == 0:
+                x_codes[n] = codes_pool.tile([P, K_GROUPS * P], U32, name="x_codes", align_bytes=64)
+                x_scales[n] = codes_pool.tile([P, K_GROUPS * P], U8, name="x_scales", align_bytes=64)
+            for piece in range(2):
+                first = (2 * h + piece) * (HALF_K // 8)
+                cols = slice(first, first + HALF_K // 8)
+                nc.vector.quantize_mx(
+                    out=x_codes[n][:, cols].bitcast(FP8X4),
+                    scales=x_scales[n][:, cols],
+                    in_=grouped[q][:, piece * (HALF_K // 2) : (piece + 1) * (HALF_K // 2)],
+                )
+
+        def first_matmul(n, cut):
+            if cut == 0:
+                h_acc[n] = h_banks.tile([P, FEAT], F32, name="h_acc")
+            cols = slice(FEATURE_CUTS[cut][0], FEATURE_CUTS[cut][1])
+            for g in range(K_GROUPS):
+                nodes = slice(g * P, (g + 1) * P)
+                nc.tensor.matmul_mx(
+                    out=h_acc[n][:, cols],
+                    lhsT=x_codes[n][:, nodes].bitcast(FP8X4),
+                    lhsT_scale=x_scales[n][:, nodes],
+                    rhs=w_codes[:, g, cols].bitcast(FP8X4),
+                    rhs_scale=w_scales[:, g, cols],
+                    start=(g == 0),
+                    stop=(g == K_GROUPS - 1),
+                )
+
+        def transpose_adj(n):
+            words = adj_raw[n][:].bitcast(F32).rearrange("i (c u p) -> i c u p", c=NODE_GROUPS, u=2)
+            bank = banks.tile([P, NODE_GROUPS, 2, P], F32, name="bank")
+            for c in range(NODE_GROUPS):
+                for u in range(2):
+                    nc.tensor.transpose(bank[:, c, u, :], words[:, c, u, :], identity[:])
+            adj_grouped[n] = adj_pool.tile([P, NODES], BF16, name="adj_grouped", align_bytes=64)
+            nc.scalar.copy(
+                out=adj_grouped[n][:].bitcast(F32).rearrange("p (c i u) -> p c i u", c=NODE_GROUPS, u=2),
+                in_=bank[:].rearrange("p c u i -> p c i u"),
+            )
+            unused = adj_pool.tile([P, NODES], BF16, name="unused")
+            nc.scalar.activation(out=unused[:], in_=adj_raw[n][:], func=ACT.Copy, accum_out=deg[:, n : n + 1])
+            nc.gpsimd.tensor_scalar_add(out=deg1[:, n : n + 1], in0=deg[:, n : n + 1], scalar1=1.0)
+            nc.gpsimd.tensor_tensor(out=dinv[:, n : n + 1], in0=deg1[:, n : n + 1], in1=minus_half[:], op=ALU.pow)
+
+        def quantise_adj(n):
+            nc.vector.quantize_mx(
+                out=adj_codes[:, n, :, :].rearrange("p c i -> p (c i)").bitcast(FP8X4),
+                scales=adj_scales[:, n, :, :].rearrange("p c i -> p (c i)"),
+                in_=adj_grouped[n][:],
+            )
+
+        def finish_h(n):
+            c, t = divmod(n, TILES_PER_GROUP)
+            nc.vector.tensor_tensor(out=hb[:, n, :], in0=h_acc[n][:], in1=spread[:, 0, :], op=ALU.add)
+            nc.vector.tensor_scalar(
+                out=hs_grouped[:, c, :, t], in0=hb[:, n, :], scalar1=dinv[:, n : n + 1], scalar2=None, op0=ALU.mult
+            )
+            if t == TILES_PER_GROUP - 1:
+                values = hs_grouped[:, c, :, :].rearrange("p f t -> p (f t)")
+                for first, last in FEATURE_CUTS:
+                    nc.vector.quantize_mx(
+                        out=hs_codes[:, c, first:last].bitcast(FP8X4),
+                        scales=hs_scales[:, c, first:last],
+                        in_=values[:, first * PACK : last * PACK],
+                    )
+
+        nc.vector.memset(warm[:], 0.0)
+        nc.scalar.activation(out=warm[:], in_=warm[:], func=ACT.Gelu)
+        nc.vector.memset(w_scales[:].rearrange("p g f -> p (g f)").bitcast(I32), 0)
+        nc.vector.memset(rows[:], 0.0)
+        nc.vector.memset(ones[:], 1.0)
+        nc.vector.memset(minus_half[:], -0.5)
+        make_identity(nc, identity[:])
+
+        for v, vector in enumerate((b1, ln_gamma, ln_beta)):
+            nc.scalar.dma_start(out=rows[0:1, v, 0:FEAT], in_=vector.rearrange("(o f) -> o f", o=1))
+
+        load_x(0)
+        load_x(1)
+        load_adj(0)
+        for quadrant in range(4):
+            nc.sync.dma_start(
+                out=w_scales[32 * quadrant : 32 * quadrant + 4, :, :].bitcast(I32),
+                in_=W1_scales[:, 4 * quadrant : 4 * quadrant + 4, :].rearrange("g r f -> r g f").bitcast(I32),
+            )
+        for g0 in range(0, K_GROUPS, 4):
+            nc.sync.dma_start(
+                out=w_codes[:, g0 : g0 + 4, :].bitcast(I32),
+                in_=W1_words[g0 : g0 + 4].rearrange("g p f t -> p g (f t)").bitcast(I32),
+            )
+        load_x(2)
+        load_adj(1)
+
+        for v in range(3):
+            bank = banks.tile([P, 512], F32, name="bank")
+            nc.tensor.matmul(out=bank[:], lhsT=ones[:], rhs=rows[:, v, :], start=True, stop=True)
+            nc.scalar.copy(out=spread[:, v, :], in_=bank[:, 0:FEAT])
+
+        def sort_and_load_next(q):
+            if q < HALVES:
+                sort_words(q)
+            if q + 3 < HALVES:
+                load_x(q + 3)
+
+        sort_and_load_next(0)
+        transpose_x(0)
+        sort_and_load_next(1)
+        transpose_x(1)
+        transpose_adj(0)
+        sort_and_load_next(2)
+        quantise_x(0)
+        sort_and_load_next(3)
+
+        for n in range(TILES):
+            more = n + 1 < TILES
+            if more:
+                transpose_x(2 * n + 2)
+            quantise_x(2 * n + 1)
+            quantise_adj(n)
+            if n > 0:
+                finish_h(n - 1)
+            sort_and_load_next(2 * n + 4)
+            first_matmul(n, 0)
+            if more:
+                transpose_x(2 * n + 3)
+                transpose_adj(n + 1)
+                if n + 2 < TILES:
+                    load_adj(n + 2)
+                quantise_x(2 * n + 2)
+            sort_and_load_next(2 * n + 5)
+            first_matmul(n, 1)
+        finish_h(TILES - 1)
+
+        agg = {}
+        summed = {}
+        gelu = {}
+        centred = {}
+
+        def second_matmul(i):
+            agg[i] = banks.tile([P, 512], F32, name="bank")
+            for first, last in FEATURE_CUTS:
+                cols = slice(first, last)
+                for c in range(NODE_GROUPS):
+                    nc.tensor.matmul_mx(
+                        out=agg[i][:, cols],
+                        lhsT=adj_codes[:, i, c, :].bitcast(FP8X4),
+                        lhsT_scale=adj_scales[:, i, c, :],
+                        rhs=hs_codes[:, c, cols].bitcast(FP8X4),
+                        rhs_scale=hs_scales[:, c, cols],
+                        start=(c == 0),
+                        stop=(c == NODE_GROUPS - 1),
+                    )
+            summed[i] = tail_pool.tile([P, FEAT], F32, name="summed")
+            nc.vector.scalar_tensor_tensor(
+                out=summed[i][:], in0=hb[:, i, :], scalar=dinv[:, i : i + 1], in1=agg[i][:, 0:FEAT],
+                op0=ALU.mult, op1=ALU.add,
+            )
+            gelu[i] = tail_pool.tile([P, FEAT], F32, name="gelu")
+            nc.scalar.activation(
+                out=gelu[i][:], in_=summed[i][:], func=ACT.Gelu, scale=dinv[:, i : i + 1],
+                accum_out=g_sum[:, i : i + 1],
+            )
+            nc.gpsimd.tensor_scalar(
+                out=minus_mean[:, i : i + 1], in0=g_sum[:, i : i + 1], scalar1=-1.0 / FEAT, scalar2=0.0,
+                op0=ALU.mult, op1=ALU.add,
+            )
+
+        def centre(i):
+            squares = tail_pool.tile([P, FEAT], F32, name="squares")
+            nc.scalar.activation(
+                out=squares[:], in_=gelu[i][:], func=ACT.Square, bias=minus_mean[:, i : i + 1], scale=1.0,
+                accum_out=sq_sum[:, i : i + 1],
+            )
+            centred[i] = tail_pool.tile([P, FEAT], F32, name="centred")
+            nc.vector.scalar_tensor_tensor(
+                out=centred[i][:], in0=gelu[i][:], scalar=minus_mean[:, i : i + 1], in1=spread[:, 1, :],
+                op0=ALU.add, op1=ALU.mult,
+            )
+            nc.gpsimd.tensor_scalar(
+                out=var_eps[:, i : i + 1], in0=sq_sum[:, i : i + 1], scalar1=1.0 / FEAT, scalar2=EPS,
+                op0=ALU.mult, op1=ALU.add,
+            )
+            nc.gpsimd.tensor_tensor(out=rstd[:, i : i + 1], in0=var_eps[:, i : i + 1], in1=minus_half[:], op=ALU.pow)
+
+        def scale_and_store(i):
+            result = tail_pool.tile([P, FEAT], F32, name="result")
+            nc.vector.scalar_tensor_tensor(
+                out=result[:], in0=centred[i][:], scalar=rstd[:, i : i + 1], in1=spread[:, 2, :],
+                op0=ALU.mult, op1=ALU.add,
+            )
+            nc.sync.dma_start(out=out_tiles[i // 2, i % 2, :, :], in_=result[:])
+
+        for step in range(TILES + 2):
+            if step < TILES:
+                second_matmul(step)
+            if 0 <= step - 1 < TILES:
+                centre(step - 1)
+            if 0 <= step - 2:
+                scale_and_store(step - 2)

@@ -32,6 +32,8 @@ BANK_GROUPS = 2
 WIDE = 256
 FEATURE_CUTS = ((0, WIDE), (WIDE, FEAT))
 
+RAW_BUFS = 5
+
 FLOPS = 2 * NODES * K * FEAT + 2 * NODES * NODES * FEAT
 
 
@@ -48,8 +50,7 @@ def tile_gcnlayer_pa_k_kernel(tc, x, adj, W1_words, W1_scales, b1, ln_gamma, ln_
     with ExitStack() as ctx:
         ctx.enter_context(tc.manual_schedule())
         keep = ctx.enter_context(tc.tile_pool(name="keep", bufs=1))
-        raw_pool = ctx.enter_context(tc.tile_pool(name="raw", bufs=3))
-        sorted_pool = ctx.enter_context(tc.tile_pool(name="sorted", bufs=4))
+        raw_pool = ctx.enter_context(tc.tile_pool(name="raw", bufs=RAW_BUFS))
         grouped_pool = ctx.enter_context(tc.tile_pool(name="grouped", bufs=3))
         codes_pool = ctx.enter_context(tc.tile_pool(name="codes", bufs=3))
         adj_pool = ctx.enter_context(tc.tile_pool(name="adj", bufs=2))
@@ -81,7 +82,6 @@ def tile_gcnlayer_pa_k_kernel(tc, x, adj, W1_words, W1_scales, b1, ln_gamma, ln_
         rstd = keep.tile([P, TILES], F32)
 
         raw = {}
-        ordered = {}
         grouped = {}
         x_codes = {}
         x_scales = {}
@@ -98,15 +98,8 @@ def tile_gcnlayer_pa_k_kernel(tc, x, adj, W1_words, W1_scales, b1, ln_gamma, ln_
             adj_raw[n] = adj_pool.tile([P, NODES], BF16, name="adj_raw")
             nc.sync.dma_start(out=adj_raw[n][:], in_=adj_tiles[n // 2, n % 2, :, :])
 
-        def sort_words(q):
-            ordered[q] = sorted_pool.tile([P, HALF_K], BF16, name="ordered")
-            nc.vector.tensor_copy(
-                out=ordered[q][:].bitcast(F32).rearrange("n (g u p) -> n g u p", g=HALF_GROUPS, u=2),
-                in_=raw[q][:].bitcast(F32).rearrange("n (g p u) -> n g u p", g=HALF_GROUPS, u=2),
-            )
-
         def transpose_x(q):
-            words = ordered[q][:].bitcast(F32).rearrange("n (g u p) -> n g u p", g=HALF_GROUPS, u=2)
+            words = raw[q][:].bitcast(F32).rearrange("n (g p u) -> n g u p", g=HALF_GROUPS, u=2)
             grouped[q] = grouped_pool.tile([P, HALF_K], BF16, name="grouped", align_bytes=64)
             pairs = grouped[q][:].bitcast(F32).rearrange("p (g n u) -> p g n u", g=HALF_GROUPS, u=2)
             for g0 in range(0, HALF_GROUPS, BANK_GROUPS):
@@ -213,44 +206,39 @@ def tile_gcnlayer_pa_k_kernel(tc, x, adj, W1_words, W1_scales, b1, ln_gamma, ln_
             )
         load_x(2)
         load_adj(1)
+        load_x(3)
+        load_x(4)
 
         for v in range(3):
             bank = banks.tile([P, 512], F32, name="bank")
             nc.tensor.matmul(out=bank[:], lhsT=ones[:], rhs=rows[:, v, :], start=True, stop=True)
             nc.scalar.copy(out=spread[:, v, :], in_=bank[:, 0:FEAT])
 
-        def sort_and_load_next(q):
-            if q < HALVES:
-                sort_words(q)
-            if q + 3 < HALVES:
-                load_x(q + 3)
+        def transpose_and_load_next(q):
+            transpose_x(q)
+            if q + RAW_BUFS < HALVES:
+                load_x(q + RAW_BUFS)
 
-        sort_and_load_next(0)
-        transpose_x(0)
-        sort_and_load_next(1)
-        transpose_x(1)
+        transpose_and_load_next(0)
+        transpose_and_load_next(1)
         transpose_adj(0)
-        sort_and_load_next(2)
         quantise_x(0)
-        sort_and_load_next(3)
 
         for n in range(TILES):
             more = n + 1 < TILES
             if more:
-                transpose_x(2 * n + 2)
+                transpose_and_load_next(2 * n + 2)
             quantise_x(2 * n + 1)
             quantise_adj(n)
             if n > 0:
                 finish_h(n - 1)
-            sort_and_load_next(2 * n + 4)
             first_matmul(n, 0)
             if more:
-                transpose_x(2 * n + 3)
+                transpose_and_load_next(2 * n + 3)
                 transpose_adj(n + 1)
                 if n + 2 < TILES:
                     load_adj(n + 2)
                 quantise_x(2 * n + 2)
-            sort_and_load_next(2 * n + 5)
             first_matmul(n, 1)
         finish_h(TILES - 1)
 

@@ -32,7 +32,7 @@ BANK_GROUPS = 2
 WIDE = 256
 FEATURE_CUTS = ((0, WIDE), (WIDE, FEAT))
 
-RAW_BUFS = 5
+NARROW_LAG = 2
 
 FLOPS = 2 * NODES * K * FEAT + 2 * NODES * NODES * FEAT
 
@@ -50,11 +50,12 @@ def tile_gcnlayer_pa_k_kernel(tc, x, adj, W1_words, W1_scales, b1, ln_gamma, ln_
     with ExitStack() as ctx:
         ctx.enter_context(tc.manual_schedule())
         keep = ctx.enter_context(tc.tile_pool(name="keep", bufs=1))
-        raw_pool = ctx.enter_context(tc.tile_pool(name="raw", bufs=RAW_BUFS))
+        raw_pool = ctx.enter_context(tc.tile_pool(name="raw", bufs=3))
+        sorted_pool = ctx.enter_context(tc.tile_pool(name="sorted", bufs=3))
         grouped_pool = ctx.enter_context(tc.tile_pool(name="grouped", bufs=3))
-        codes_pool = ctx.enter_context(tc.tile_pool(name="codes", bufs=3))
+        codes_pool = ctx.enter_context(tc.tile_pool(name="codes", bufs=NARROW_LAG + 2))
         adj_pool = ctx.enter_context(tc.tile_pool(name="adj", bufs=2))
-        tail_pool = ctx.enter_context(tc.tile_pool(name="tail", bufs=3))
+        tail_pool = ctx.enter_context(tc.tile_pool(name="tail", bufs=4))
         banks = ctx.enter_context(tc.psum_pool(name="banks", bufs=6))
         h_banks = ctx.enter_context(tc.psum_pool(name="h_banks", bufs=2))
 
@@ -75,13 +76,17 @@ def tile_gcnlayer_pa_k_kernel(tc, x, adj, W1_words, W1_scales, b1, ln_gamma, ln_
         deg = keep.tile([P, TILES], F32)
         deg1 = keep.tile([P, TILES], F32)
         dinv = keep.tile([P, TILES], F32)
-        g_sum = keep.tile([P, TILES], F32)
+        gelu = keep.tile([P, TILES, FEAT], F32)
+        wide_sum = keep.tile([P, TILES], F32)
+        narrow_sum = keep.tile([P, TILES], F32)
+        wide_share = keep.tile([P, TILES], F32)
         minus_mean = keep.tile([P, TILES], F32)
         sq_sum = keep.tile([P, TILES], F32)
         var_eps = keep.tile([P, TILES], F32)
         rstd = keep.tile([P, TILES], F32)
 
         raw = {}
+        ordered = {}
         grouped = {}
         x_codes = {}
         x_scales = {}
@@ -98,8 +103,15 @@ def tile_gcnlayer_pa_k_kernel(tc, x, adj, W1_words, W1_scales, b1, ln_gamma, ln_
             adj_raw[n] = adj_pool.tile([P, NODES], BF16, name="adj_raw")
             nc.sync.dma_start(out=adj_raw[n][:], in_=adj_tiles[n // 2, n % 2, :, :])
 
+        def sort_words(q):
+            ordered[q] = sorted_pool.tile([P, HALF_K], BF16, name="ordered")
+            nc.vector.tensor_copy(
+                out=ordered[q][:].bitcast(F32).rearrange("n (g u p) -> n g u p", g=HALF_GROUPS, u=2),
+                in_=raw[q][:].bitcast(F32).rearrange("n (g p u) -> n g u p", g=HALF_GROUPS, u=2),
+            )
+
         def transpose_x(q):
-            words = raw[q][:].bitcast(F32).rearrange("n (g p u) -> n g u p", g=HALF_GROUPS, u=2)
+            words = ordered[q][:].bitcast(F32).rearrange("n (g u p) -> n g u p", g=HALF_GROUPS, u=2)
             grouped[q] = grouped_pool.tile([P, HALF_K], BF16, name="grouped", align_bytes=64)
             pairs = grouped[q][:].bitcast(F32).rearrange("p (g n u) -> p g n u", g=HALF_GROUPS, u=2)
             for g0 in range(0, HALF_GROUPS, BANK_GROUPS):
@@ -127,13 +139,13 @@ def tile_gcnlayer_pa_k_kernel(tc, x, adj, W1_words, W1_scales, b1, ln_gamma, ln_
                 )
 
         def first_matmul(n, cut):
-            if cut == 0:
-                h_acc[n] = h_banks.tile([P, FEAT], F32, name="h_acc")
-            cols = slice(FEATURE_CUTS[cut][0], FEATURE_CUTS[cut][1])
+            first, last = FEATURE_CUTS[cut]
+            h_acc[n, cut] = h_banks.tile([P, WIDE], F32, name="h_acc")
+            cols = slice(first, last)
             for g in range(K_GROUPS):
                 nodes = slice(g * P, (g + 1) * P)
                 nc.tensor.matmul_mx(
-                    out=h_acc[n][:, cols],
+                    out=h_acc[n, cut][:, 0 : last - first],
                     lhsT=x_codes[n][:, nodes].bitcast(FP8X4),
                     lhsT_scale=x_scales[n][:, nodes],
                     rhs=w_codes[:, g, cols].bitcast(FP8X4),
@@ -153,6 +165,8 @@ def tile_gcnlayer_pa_k_kernel(tc, x, adj, W1_words, W1_scales, b1, ln_gamma, ln_
                 out=adj_grouped[n][:].bitcast(F32).rearrange("p (c i u) -> p c i u", c=NODE_GROUPS, u=2),
                 in_=bank[:].rearrange("p c u i -> p c i u"),
             )
+
+        def degree(n):
             unused = adj_pool.tile([P, NODES], BF16, name="unused")
             nc.scalar.activation(out=unused[:], in_=adj_raw[n][:], func=ACT.Copy, accum_out=deg[:, n : n + 1])
             nc.gpsimd.tensor_scalar_add(out=deg1[:, n : n + 1], in0=deg[:, n : n + 1], scalar1=1.0)
@@ -165,20 +179,31 @@ def tile_gcnlayer_pa_k_kernel(tc, x, adj, W1_words, W1_scales, b1, ln_gamma, ln_
                 in_=adj_grouped[n][:],
             )
 
-        def finish_h(n):
+        def finish_h(n, cut):
             c, t = divmod(n, TILES_PER_GROUP)
-            nc.vector.tensor_tensor(out=hb[:, n, :], in0=h_acc[n][:], in1=spread[:, 0, :], op=ALU.add)
+            first, last = FEATURE_CUTS[cut]
+            nc.vector.tensor_tensor(
+                out=hb[:, n, first:last], in0=h_acc[n, cut][:, 0 : last - first], in1=spread[:, 0, first:last], op=ALU.add
+            )
             nc.vector.tensor_scalar(
-                out=hs_grouped[:, c, :, t], in0=hb[:, n, :], scalar1=dinv[:, n : n + 1], scalar2=None, op0=ALU.mult
+                out=hs_grouped[:, c, first:last, t], in0=hb[:, n, first:last], scalar1=dinv[:, n : n + 1],
+                scalar2=None, op0=ALU.mult,
             )
             if t == TILES_PER_GROUP - 1:
-                values = hs_grouped[:, c, :, :].rearrange("p f t -> p (f t)")
-                for first, last in FEATURE_CUTS:
-                    nc.vector.quantize_mx(
-                        out=hs_codes[:, c, first:last].bitcast(FP8X4),
-                        scales=hs_scales[:, c, first:last],
-                        in_=values[:, first * PACK : last * PACK],
-                    )
+                nc.vector.quantize_mx(
+                    out=hs_codes[:, c, first:last].bitcast(FP8X4),
+                    scales=hs_scales[:, c, first:last],
+                    in_=hs_grouped[:, c, first:last, :].rearrange("p f t -> p (f t)"),
+                )
+
+        def load_w(cut, pieces):
+            first, last = FEATURE_CUTS[cut]
+            step = K_GROUPS // pieces
+            for g0 in range(0, K_GROUPS, step):
+                nc.sync.dma_start(
+                    out=w_codes[:, g0 : g0 + step, first:last].bitcast(I32),
+                    in_=W1_words[g0 : g0 + step, :, first:last, :].rearrange("g p f t -> p g (f t)").bitcast(I32),
+                )
 
         nc.vector.memset(warm[:], 0.0)
         nc.scalar.activation(out=warm[:], in_=warm[:], func=ACT.Gelu)
@@ -194,97 +219,92 @@ def tile_gcnlayer_pa_k_kernel(tc, x, adj, W1_words, W1_scales, b1, ln_gamma, ln_
         load_x(0)
         load_x(1)
         load_adj(0)
+        load_x(2)
         for quadrant in range(4):
             nc.sync.dma_start(
                 out=w_scales[32 * quadrant : 32 * quadrant + 4, :, :].bitcast(I32),
                 in_=W1_scales[:, 4 * quadrant : 4 * quadrant + 4, :].rearrange("g r f -> r g f").bitcast(I32),
             )
-        for g0 in range(0, K_GROUPS, 4):
-            nc.sync.dma_start(
-                out=w_codes[:, g0 : g0 + 4, :].bitcast(I32),
-                in_=W1_words[g0 : g0 + 4].rearrange("g p f t -> p g (f t)").bitcast(I32),
-            )
-        load_x(2)
-        load_adj(1)
-        load_x(3)
-        load_x(4)
+        load_w(0, 2)
 
+        def sort_and_load_next(q):
+            if q < HALVES:
+                sort_words(q)
+            if q + 3 < HALVES:
+                load_x(q + 3)
+
+        sort_and_load_next(0)
+        transpose_x(0)
+        sort_and_load_next(1)
+        transpose_x(1)
+        degree(0)
+        transpose_adj(0)
         for v in range(3):
             bank = banks.tile([P, 512], F32, name="bank")
             nc.tensor.matmul(out=bank[:], lhsT=ones[:], rhs=rows[:, v, :], start=True, stop=True)
             nc.scalar.copy(out=spread[:, v, :], in_=bank[:, 0:FEAT])
-
-        def transpose_and_load_next(q):
-            transpose_x(q)
-            if q + RAW_BUFS < HALVES:
-                load_x(q + RAW_BUFS)
-
-        transpose_and_load_next(0)
-        transpose_and_load_next(1)
-        transpose_adj(0)
+        sort_and_load_next(2)
+        load_adj(1)
+        load_w(1, 1)
         quantise_x(0)
+        sort_and_load_next(3)
 
         for n in range(TILES):
             more = n + 1 < TILES
             if more:
-                transpose_and_load_next(2 * n + 2)
+                transpose_x(2 * n + 2)
+                degree(n + 1)
             quantise_x(2 * n + 1)
             quantise_adj(n)
-            if n > 0:
-                finish_h(n - 1)
+            if n - 1 - NARROW_LAG >= 0:
+                finish_h(n - 1 - NARROW_LAG, 1)
+            sort_and_load_next(2 * n + 4)
             first_matmul(n, 0)
             if more:
-                transpose_and_load_next(2 * n + 3)
+                transpose_x(2 * n + 3)
                 transpose_adj(n + 1)
                 if n + 2 < TILES:
                     load_adj(n + 2)
                 quantise_x(2 * n + 2)
-            first_matmul(n, 1)
-        finish_h(TILES - 1)
+            finish_h(n, 0)
+            sort_and_load_next(2 * n + 5)
+            if n - NARROW_LAG >= 0:
+                first_matmul(n - NARROW_LAG, 1)
 
-        agg = {}
-        summed = {}
-        gelu = {}
         centred = {}
 
-        def second_matmul(i):
-            agg[i] = banks.tile([P, 512], F32, name="bank")
-            for first, last in FEATURE_CUTS:
-                cols = slice(first, last)
-                for c in range(NODE_GROUPS):
-                    nc.tensor.matmul_mx(
-                        out=agg[i][:, cols],
-                        lhsT=adj_codes[:, i, c, :].bitcast(FP8X4),
-                        lhsT_scale=adj_scales[:, i, c, :],
-                        rhs=hs_codes[:, c, cols].bitcast(FP8X4),
-                        rhs_scale=hs_scales[:, c, cols],
-                        start=(c == 0),
-                        stop=(c == NODE_GROUPS - 1),
-                    )
-            summed[i] = tail_pool.tile([P, FEAT], F32, name="summed")
+        def second_matmul(i, cut, sums):
+            first, last = FEATURE_CUTS[cut]
+            agg = banks.tile([P, 512], F32, name="bank")
+            for c in range(NODE_GROUPS):
+                nc.tensor.matmul_mx(
+                    out=agg[:, 0 : last - first],
+                    lhsT=adj_codes[:, i, c, :].bitcast(FP8X4),
+                    lhsT_scale=adj_scales[:, i, c, :],
+                    rhs=hs_codes[:, c, first:last].bitcast(FP8X4),
+                    rhs_scale=hs_scales[:, c, first:last],
+                    start=(c == 0),
+                    stop=(c == NODE_GROUPS - 1),
+                )
+            summed = tail_pool.tile([P, WIDE], F32, name="summed")
             nc.vector.scalar_tensor_tensor(
-                out=summed[i][:], in0=hb[:, i, :], scalar=dinv[:, i : i + 1], in1=agg[i][:, 0:FEAT],
-                op0=ALU.mult, op1=ALU.add,
+                out=summed[:, 0 : last - first], in0=hb[:, i, first:last], scalar=dinv[:, i : i + 1],
+                in1=agg[:, 0 : last - first], op0=ALU.mult, op1=ALU.add,
             )
-            gelu[i] = tail_pool.tile([P, FEAT], F32, name="gelu")
             nc.scalar.activation(
-                out=gelu[i][:], in_=summed[i][:], func=ACT.Gelu, scale=dinv[:, i : i + 1],
-                accum_out=g_sum[:, i : i + 1],
-            )
-            nc.gpsimd.tensor_scalar(
-                out=minus_mean[:, i : i + 1], in0=g_sum[:, i : i + 1], scalar1=-1.0 / FEAT, scalar2=0.0,
-                op0=ALU.mult, op1=ALU.add,
+                out=gelu[:, i, first:last], in_=summed[:, 0 : last - first], func=ACT.Gelu,
+                scale=dinv[:, i : i + 1], accum_out=sums[:, i : i + 1],
             )
 
         def centre(i):
             squares = tail_pool.tile([P, FEAT], F32, name="squares")
             nc.scalar.activation(
-                out=squares[:], in_=gelu[i][:], func=ACT.Square, bias=minus_mean[:, i : i + 1], scale=1.0,
+                out=squares[:], in_=gelu[:, i, :], func=ACT.Square, bias=minus_mean[:, i : i + 1], scale=1.0,
                 accum_out=sq_sum[:, i : i + 1],
             )
             centred[i] = tail_pool.tile([P, FEAT], F32, name="centred")
             nc.vector.scalar_tensor_tensor(
-                out=centred[i][:], in0=gelu[i][:], scalar=minus_mean[:, i : i + 1], in1=spread[:, 1, :],
+                out=centred[i][:], in0=gelu[:, i, :], scalar=minus_mean[:, i : i + 1], in1=spread[:, 1, :],
                 op0=ALU.add, op1=ALU.mult,
             )
             nc.gpsimd.tensor_scalar(
@@ -301,10 +321,27 @@ def tile_gcnlayer_pa_k_kernel(tc, x, adj, W1_words, W1_scales, b1, ln_gamma, ln_
             )
             nc.sync.dma_start(out=out_tiles[i // 2, i % 2, :, :], in_=result[:])
 
-        for step in range(TILES + 2):
+        first_matmul(TILES - NARROW_LAG, 1)
+        finish_h(TILES - 1 - NARROW_LAG, 1)
+        for i in range(TILES):
+            second_matmul(i, 0, wide_sum)
+            nc.gpsimd.tensor_scalar(
+                out=wide_share[:, i : i + 1], in0=wide_sum[:, i : i + 1], scalar1=-1.0 / FEAT, scalar2=0.0,
+                op0=ALU.mult, op1=ALU.add,
+            )
+        for n in range(TILES - NARROW_LAG, TILES):
+            if n + 1 < TILES:
+                first_matmul(n + 1, 1)
+            finish_h(n, 1)
+
+        for step in range(TILES + 3):
             if step < TILES:
-                second_matmul(step)
+                second_matmul(step, 1, narrow_sum)
+                nc.gpsimd.tensor_scalar(
+                    out=minus_mean[:, step : step + 1], in0=narrow_sum[:, step : step + 1], scalar1=-1.0 / FEAT,
+                    scalar2=wide_share[:, step : step + 1], op0=ALU.mult, op1=ALU.add,
+                )
             if 0 <= step - 1 < TILES:
                 centre(step - 1)
-            if 0 <= step - 2:
-                scale_and_store(step - 2)
+            if 0 <= step - 3:
+                scale_and_store(step - 3)

@@ -32,8 +32,6 @@ BANK_GROUPS = 2
 WIDE = 256
 FEATURE_CUTS = ((0, WIDE), (WIDE, FEAT))
 
-NARROW_LAG = 2
-
 FLOPS = 2 * NODES * K * FEAT + 2 * NODES * NODES * FEAT
 
 
@@ -51,18 +49,18 @@ def tile_gcnlayer_pa_k_kernel(tc, x, adj, W1_words, W1_scales, b1, ln_gamma, ln_
         ctx.enter_context(tc.manual_schedule())
         keep = ctx.enter_context(tc.tile_pool(name="keep", bufs=1))
         raw_pool = ctx.enter_context(tc.tile_pool(name="raw", bufs=3))
-        sorted_pool = ctx.enter_context(tc.tile_pool(name="sorted", bufs=3))
+        sorted_pool = ctx.enter_context(tc.tile_pool(name="sorted", bufs=4))
         grouped_pool = ctx.enter_context(tc.tile_pool(name="grouped", bufs=3))
-        codes_pool = ctx.enter_context(tc.tile_pool(name="codes", bufs=NARROW_LAG + 2))
+        codes_pool = ctx.enter_context(tc.tile_pool(name="codes", bufs=3))
         adj_pool = ctx.enter_context(tc.tile_pool(name="adj", bufs=2))
-        tail_pool = ctx.enter_context(tc.tile_pool(name="tail", bufs=4))
+        tail_pool = ctx.enter_context(tc.tile_pool(name="tail", bufs=3))
         banks = ctx.enter_context(tc.psum_pool(name="banks", bufs=6))
         h_banks = ctx.enter_context(tc.psum_pool(name="h_banks", bufs=2))
 
         identity = keep.tile([P, P], F32)
         ones = keep.tile([P, P], BF16)
         rows = keep.tile([P, 3, 512], BF16)
-        spread = keep.tile([P, 3, FEAT], F32)
+        b1_spread = keep.tile([P, FEAT], F32)
         minus_half = keep.tile([P, 1], F32)
         warm = keep.tile([P, 1], F32)
         w_codes = keep.tile([P, K_GROUPS, FEAT], U32, align_bytes=64)
@@ -76,10 +74,7 @@ def tile_gcnlayer_pa_k_kernel(tc, x, adj, W1_words, W1_scales, b1, ln_gamma, ln_
         deg = keep.tile([P, TILES], F32)
         deg1 = keep.tile([P, TILES], F32)
         dinv = keep.tile([P, TILES], F32)
-        gelu = keep.tile([P, TILES, FEAT], F32)
-        wide_sum = keep.tile([P, TILES], F32)
-        narrow_sum = keep.tile([P, TILES], F32)
-        wide_share = keep.tile([P, TILES], F32)
+        g_sum = keep.tile([P, TILES], F32)
         minus_mean = keep.tile([P, TILES], F32)
         sq_sum = keep.tile([P, TILES], F32)
         var_eps = keep.tile([P, TILES], F32)
@@ -139,13 +134,13 @@ def tile_gcnlayer_pa_k_kernel(tc, x, adj, W1_words, W1_scales, b1, ln_gamma, ln_
                 )
 
         def first_matmul(n, cut):
-            first, last = FEATURE_CUTS[cut]
-            h_acc[n, cut] = h_banks.tile([P, WIDE], F32, name="h_acc")
-            cols = slice(first, last)
+            if cut == 0:
+                h_acc[n] = h_banks.tile([P, 512], F32, name="h_acc")
+            cols = slice(FEATURE_CUTS[cut][0], FEATURE_CUTS[cut][1])
             for g in range(K_GROUPS):
                 nodes = slice(g * P, (g + 1) * P)
                 nc.tensor.matmul_mx(
-                    out=h_acc[n, cut][:, 0 : last - first],
+                    out=h_acc[n][:, cols],
                     lhsT=x_codes[n][:, nodes].bitcast(FP8X4),
                     lhsT_scale=x_scales[n][:, nodes],
                     rhs=w_codes[:, g, cols].bitcast(FP8X4),
@@ -165,11 +160,9 @@ def tile_gcnlayer_pa_k_kernel(tc, x, adj, W1_words, W1_scales, b1, ln_gamma, ln_
                 out=adj_grouped[n][:].bitcast(F32).rearrange("p (c i u) -> p c i u", c=NODE_GROUPS, u=2),
                 in_=bank[:].rearrange("p c u i -> p c i u"),
             )
-
-        def degree(n):
             unused = adj_pool.tile([P, NODES], BF16, name="unused")
             nc.scalar.activation(out=unused[:], in_=adj_raw[n][:], func=ACT.Copy, accum_out=deg[:, n : n + 1])
-            nc.gpsimd.tensor_scalar_add(out=deg1[:, n : n + 1], in0=deg[:, n : n + 1], scalar1=1.0)
+            nc.scalar.activation(out=deg1[:, n : n + 1], in_=deg[:, n : n + 1], func=ACT.Copy, bias=1.0)
             nc.gpsimd.tensor_tensor(out=dinv[:, n : n + 1], in0=deg1[:, n : n + 1], in1=minus_half[:], op=ALU.pow)
 
         def quantise_adj(n):
@@ -179,31 +172,20 @@ def tile_gcnlayer_pa_k_kernel(tc, x, adj, W1_words, W1_scales, b1, ln_gamma, ln_
                 in_=adj_grouped[n][:],
             )
 
-        def finish_h(n, cut):
+        def finish_h(n):
             c, t = divmod(n, TILES_PER_GROUP)
-            first, last = FEATURE_CUTS[cut]
-            nc.vector.tensor_tensor(
-                out=hb[:, n, first:last], in0=h_acc[n, cut][:, 0 : last - first], in1=spread[:, 0, first:last], op=ALU.add
-            )
+            nc.vector.tensor_tensor(out=hb[:, n, :], in0=h_acc[n][:, 0:FEAT], in1=b1_spread[:], op=ALU.add)
             nc.vector.tensor_scalar(
-                out=hs_grouped[:, c, first:last, t], in0=hb[:, n, first:last], scalar1=dinv[:, n : n + 1],
-                scalar2=None, op0=ALU.mult,
+                out=hs_grouped[:, c, :, t], in0=hb[:, n, :], scalar1=dinv[:, n : n + 1], scalar2=None, op0=ALU.mult
             )
             if t == TILES_PER_GROUP - 1:
-                nc.vector.quantize_mx(
-                    out=hs_codes[:, c, first:last].bitcast(FP8X4),
-                    scales=hs_scales[:, c, first:last],
-                    in_=hs_grouped[:, c, first:last, :].rearrange("p f t -> p (f t)"),
-                )
-
-        def load_w(cut, pieces):
-            first, last = FEATURE_CUTS[cut]
-            step = K_GROUPS // pieces
-            for g0 in range(0, K_GROUPS, step):
-                nc.sync.dma_start(
-                    out=w_codes[:, g0 : g0 + step, first:last].bitcast(I32),
-                    in_=W1_words[g0 : g0 + step, :, first:last, :].rearrange("g p f t -> p g (f t)").bitcast(I32),
-                )
+                values = hs_grouped[:, c, :, :].rearrange("p f t -> p (f t)")
+                for first, last in FEATURE_CUTS:
+                    nc.vector.quantize_mx(
+                        out=hs_codes[:, c, first:last].bitcast(FP8X4),
+                        scales=hs_scales[:, c, first:last],
+                        in_=values[:, first * PACK : last * PACK],
+                    )
 
         nc.vector.memset(warm[:], 0.0)
         nc.scalar.activation(out=warm[:], in_=warm[:], func=ACT.Gelu)
@@ -219,13 +201,18 @@ def tile_gcnlayer_pa_k_kernel(tc, x, adj, W1_words, W1_scales, b1, ln_gamma, ln_
         load_x(0)
         load_x(1)
         load_adj(0)
-        load_x(2)
         for quadrant in range(4):
             nc.sync.dma_start(
                 out=w_scales[32 * quadrant : 32 * quadrant + 4, :, :].bitcast(I32),
                 in_=W1_scales[:, 4 * quadrant : 4 * quadrant + 4, :].rearrange("g r f -> r g f").bitcast(I32),
             )
-        load_w(0, 2)
+        for g0 in range(0, K_GROUPS, 4):
+            nc.sync.dma_start(
+                out=w_codes[:, g0 : g0 + 4, :].bitcast(I32),
+                in_=W1_words[g0 : g0 + 4].rearrange("g p f t -> p g (f t)").bitcast(I32),
+            )
+        load_x(2)
+        load_adj(1)
 
         def sort_and_load_next(q):
             if q < HALVES:
@@ -237,15 +224,11 @@ def tile_gcnlayer_pa_k_kernel(tc, x, adj, W1_words, W1_scales, b1, ln_gamma, ln_
         transpose_x(0)
         sort_and_load_next(1)
         transpose_x(1)
-        degree(0)
         transpose_adj(0)
-        for v in range(3):
-            bank = banks.tile([P, 512], F32, name="bank")
-            nc.tensor.matmul(out=bank[:], lhsT=ones[:], rhs=rows[:, v, :], start=True, stop=True)
-            nc.scalar.copy(out=spread[:, v, :], in_=bank[:, 0:FEAT])
+        bank = banks.tile([P, 512], F32, name="bank")
+        nc.tensor.matmul(out=bank[:], lhsT=ones[:], rhs=rows[:, 0, :], start=True, stop=True)
+        nc.scalar.copy(out=b1_spread[:], in_=bank[:, 0:FEAT])
         sort_and_load_next(2)
-        load_adj(1)
-        load_w(1, 1)
         quantise_x(0)
         sort_and_load_next(3)
 
@@ -253,11 +236,10 @@ def tile_gcnlayer_pa_k_kernel(tc, x, adj, W1_words, W1_scales, b1, ln_gamma, ln_
             more = n + 1 < TILES
             if more:
                 transpose_x(2 * n + 2)
-                degree(n + 1)
             quantise_x(2 * n + 1)
             quantise_adj(n)
-            if n - 1 - NARROW_LAG >= 0:
-                finish_h(n - 1 - NARROW_LAG, 1)
+            if n > 0:
+                finish_h(n - 1)
             sort_and_load_next(2 * n + 4)
             first_matmul(n, 0)
             if more:
@@ -266,82 +248,69 @@ def tile_gcnlayer_pa_k_kernel(tc, x, adj, W1_words, W1_scales, b1, ln_gamma, ln_
                 if n + 2 < TILES:
                     load_adj(n + 2)
                 quantise_x(2 * n + 2)
-            finish_h(n, 0)
             sort_and_load_next(2 * n + 5)
-            if n - NARROW_LAG >= 0:
-                first_matmul(n - NARROW_LAG, 1)
+            first_matmul(n, 1)
+        finish_h(TILES - 1)
 
+        gamma_spread = h_banks.tile([P, 512], F32, name="h_acc")
+        nc.tensor.matmul(out=gamma_spread[:], lhsT=ones[:], rhs=rows[:, 1, :], start=True, stop=True)
+        beta_spread = h_banks.tile([P, 512], F32, name="h_acc")
+        nc.tensor.matmul(out=beta_spread[:], lhsT=ones[:], rhs=rows[:, 2, :], start=True, stop=True)
+
+        gelu = {}
         centred = {}
 
-        def second_matmul(i, cut, sums):
-            first, last = FEATURE_CUTS[cut]
+        def second_matmul(i):
+            one = slice(i, i + 1)
             agg = banks.tile([P, 512], F32, name="bank")
-            for c in range(NODE_GROUPS):
-                nc.tensor.matmul_mx(
-                    out=agg[:, 0 : last - first],
-                    lhsT=adj_codes[:, i, c, :].bitcast(FP8X4),
-                    lhsT_scale=adj_scales[:, i, c, :],
-                    rhs=hs_codes[:, c, first:last].bitcast(FP8X4),
-                    rhs_scale=hs_scales[:, c, first:last],
-                    start=(c == 0),
-                    stop=(c == NODE_GROUPS - 1),
-                )
-            summed = tail_pool.tile([P, WIDE], F32, name="summed")
+            for first, last in FEATURE_CUTS:
+                cols = slice(first, last)
+                for c in range(NODE_GROUPS):
+                    nc.tensor.matmul_mx(
+                        out=agg[:, cols],
+                        lhsT=adj_codes[:, i, c, :].bitcast(FP8X4),
+                        lhsT_scale=adj_scales[:, i, c, :],
+                        rhs=hs_codes[:, c, cols].bitcast(FP8X4),
+                        rhs_scale=hs_scales[:, c, cols],
+                        start=(c == 0),
+                        stop=(c == NODE_GROUPS - 1),
+                    )
+            summed = tail_pool.tile([P, FEAT], F32, name="summed")
             nc.vector.scalar_tensor_tensor(
-                out=summed[:, 0 : last - first], in0=hb[:, i, first:last], scalar=dinv[:, i : i + 1],
-                in1=agg[:, 0 : last - first], op0=ALU.mult, op1=ALU.add,
+                out=summed[:], in0=hb[:, i, :], scalar=dinv[:, one], in1=agg[:, 0:FEAT], op0=ALU.mult, op1=ALU.add
             )
+            gelu[i] = tail_pool.tile([P, FEAT], F32, name="gelu")
             nc.scalar.activation(
-                out=gelu[:, i, first:last], in_=summed[:, 0 : last - first], func=ACT.Gelu,
-                scale=dinv[:, i : i + 1], accum_out=sums[:, i : i + 1],
+                out=gelu[i][:], in_=summed[:], func=ACT.Gelu, scale=dinv[:, one], accum_out=g_sum[:, one]
             )
-
-        def centre(i):
+            nc.scalar.activation(out=minus_mean[:, one], in_=g_sum[:, one], func=ACT.Copy, scale=-1.0 / FEAT)
             squares = tail_pool.tile([P, FEAT], F32, name="squares")
             nc.scalar.activation(
-                out=squares[:], in_=gelu[:, i, :], func=ACT.Square, bias=minus_mean[:, i : i + 1], scale=1.0,
-                accum_out=sq_sum[:, i : i + 1],
+                out=squares[:], in_=gelu[i][:], func=ACT.Square, bias=minus_mean[:, one], scale=1.0,
+                accum_out=sq_sum[:, one],
             )
+            nc.scalar.activation(out=var_eps[:, one], in_=sq_sum[:, one], func=ACT.Copy, scale=1.0 / FEAT, bias=EPS)
+            nc.gpsimd.tensor_tensor(out=rstd[:, one], in0=var_eps[:, one], in1=minus_half[:], op=ALU.pow)
+
+        def centre(i):
             centred[i] = tail_pool.tile([P, FEAT], F32, name="centred")
             nc.vector.scalar_tensor_tensor(
-                out=centred[i][:], in0=gelu[:, i, :], scalar=minus_mean[:, i : i + 1], in1=spread[:, 1, :],
+                out=centred[i][:], in0=gelu[i][:], scalar=minus_mean[:, i : i + 1], in1=gamma_spread[:, 0:FEAT],
                 op0=ALU.add, op1=ALU.mult,
             )
-            nc.gpsimd.tensor_scalar(
-                out=var_eps[:, i : i + 1], in0=sq_sum[:, i : i + 1], scalar1=1.0 / FEAT, scalar2=EPS,
-                op0=ALU.mult, op1=ALU.add,
-            )
-            nc.gpsimd.tensor_tensor(out=rstd[:, i : i + 1], in0=var_eps[:, i : i + 1], in1=minus_half[:], op=ALU.pow)
 
         def scale_and_store(i):
             result = tail_pool.tile([P, FEAT], F32, name="result")
             nc.vector.scalar_tensor_tensor(
-                out=result[:], in0=centred[i][:], scalar=rstd[:, i : i + 1], in1=spread[:, 2, :],
+                out=result[:], in0=centred[i][:], scalar=rstd[:, i : i + 1], in1=beta_spread[:, 0:FEAT],
                 op0=ALU.mult, op1=ALU.add,
             )
             nc.sync.dma_start(out=out_tiles[i // 2, i % 2, :, :], in_=result[:])
 
-        first_matmul(TILES - NARROW_LAG, 1)
-        finish_h(TILES - 1 - NARROW_LAG, 1)
-        for i in range(TILES):
-            second_matmul(i, 0, wide_sum)
-            nc.gpsimd.tensor_scalar(
-                out=wide_share[:, i : i + 1], in0=wide_sum[:, i : i + 1], scalar1=-1.0 / FEAT, scalar2=0.0,
-                op0=ALU.mult, op1=ALU.add,
-            )
-        for n in range(TILES - NARROW_LAG, TILES):
-            if n + 1 < TILES:
-                first_matmul(n + 1, 1)
-            finish_h(n, 1)
-
-        for step in range(TILES + 3):
+        for step in range(TILES + 2):
             if step < TILES:
-                second_matmul(step, 1, narrow_sum)
-                nc.gpsimd.tensor_scalar(
-                    out=minus_mean[:, step : step + 1], in0=narrow_sum[:, step : step + 1], scalar1=-1.0 / FEAT,
-                    scalar2=wide_share[:, step : step + 1], op0=ALU.mult, op1=ALU.add,
-                )
+                second_matmul(step)
             if 0 <= step - 1 < TILES:
                 centre(step - 1)
-            if 0 <= step - 3:
-                scale_and_store(step - 3)
+            if 0 <= step - 2:
+                scale_and_store(step - 2)

@@ -24,13 +24,19 @@ TILES = NODES // P
 NODE_GROUPS = NODES // K_PASS
 TILES_PER_GROUP = TILES // NODE_GROUPS
 K_GROUPS = K // K_PASS
-HALF_GROUPS = K_GROUPS // 2
-HALF_K = HALF_GROUPS * K_PASS
-HALF_WORDS = HALF_K // 2
-HALVES = 2 * TILES
+QUARTERS = 4
+UNIT_GROUPS = K_GROUPS // QUARTERS
+UNIT_K = K // QUARTERS
+UNIT_COLS = UNIT_GROUPS * P
 BANK_GROUPS = 2
 WIDE = 256
 FEATURE_CUTS = ((0, WIDE), (WIDE, FEAT))
+
+STEPS = [((0, q), (1, q)) for q in range(QUARTERS)] + [
+    ((n, q), (n, q + 1)) for n in range(2, TILES) for q in (0, 2)
+]
+LAST_STEP = {n: max(s for s, units in enumerate(STEPS) if n in (units[0][0], units[1][0])) for n in range(TILES)}
+RAW_BUFS = 5
 
 FLOPS = 2 * NODES * K * FEAT + 2 * NODES * NODES * FEAT
 
@@ -48,14 +54,15 @@ def tile_gcnlayer_pa_k_kernel(tc, x, adj, W1_words, W1_scales, b1, ln_gamma, ln_
     with ExitStack() as ctx:
         ctx.enter_context(tc.manual_schedule())
         keep = ctx.enter_context(tc.tile_pool(name="keep", bufs=1))
-        raw_pool = ctx.enter_context(tc.tile_pool(name="raw", bufs=3))
-        sorted_pool = ctx.enter_context(tc.tile_pool(name="sorted", bufs=4))
+        raw_pool = ctx.enter_context(tc.tile_pool(name="raw", bufs=RAW_BUFS))
+        sorted_pool = ctx.enter_context(tc.tile_pool(name="sorted", bufs=3))
         grouped_pool = ctx.enter_context(tc.tile_pool(name="grouped", bufs=3))
         codes_pool = ctx.enter_context(tc.tile_pool(name="codes", bufs=3))
+        adj_raw_pool = ctx.enter_context(tc.tile_pool(name="adj_raw", bufs=4))
         adj_pool = ctx.enter_context(tc.tile_pool(name="adj", bufs=2))
-        tail_pool = ctx.enter_context(tc.tile_pool(name="tail", bufs=3))
-        banks = ctx.enter_context(tc.psum_pool(name="banks", bufs=6))
-        h_banks = ctx.enter_context(tc.psum_pool(name="h_banks", bufs=2))
+        tail_pool = ctx.enter_context(tc.tile_pool(name="tail", bufs=4))
+        banks = ctx.enter_context(tc.psum_pool(name="banks", bufs=4))
+        h_banks = ctx.enter_context(tc.psum_pool(name="h_banks", bufs=4))
 
         identity = keep.tile([P, P], F32)
         ones = keep.tile([P, P], BF16)
@@ -72,7 +79,6 @@ def tile_gcnlayer_pa_k_kernel(tc, x, adj, W1_words, W1_scales, b1, ln_gamma, ln_
         hs_codes = keep.tile([P, NODE_GROUPS, FEAT], U32, align_bytes=64)
         hs_scales = keep.tile([P, NODE_GROUPS, FEAT], U8, align_bytes=64)
         deg = keep.tile([P, TILES], F32)
-        deg1 = keep.tile([P, TILES], F32)
         dinv = keep.tile([P, TILES], F32)
         g_sum = keep.tile([P, TILES], F32)
         minus_mean = keep.tile([P, TILES], F32)
@@ -89,65 +95,86 @@ def tile_gcnlayer_pa_k_kernel(tc, x, adj, W1_words, W1_scales, b1, ln_gamma, ln_
         adj_grouped = {}
         h_acc = {}
 
-        def load_x(q):
-            n, h = divmod(q, 2)
-            raw[q] = raw_pool.tile([P, HALF_K], BF16, name="raw")
-            nc.sync.dma_start(out=raw[q][:], in_=x_tiles[n // 2, n % 2, :, h * HALF_K : (h + 1) * HALF_K])
+        def load_step(s):
+            raw[s] = raw_pool.tile([P, 2, UNIT_K], BF16, name="raw")
+            (n0, q0), (n1, q1) = STEPS[s]
+            if n0 == n1:
+                nc.sync.dma_start(
+                    out=raw[s][:].rearrange("n a k -> n (a k)"),
+                    in_=x_tiles[n0 // 2, n0 % 2, :, q0 * UNIT_K : (q1 + 1) * UNIT_K],
+                )
+            else:
+                for a, (n, q) in enumerate(STEPS[s]):
+                    nc.sync.dma_start(
+                        out=raw[s][:, a, :], in_=x_tiles[n // 2, n % 2, :, q * UNIT_K : (q + 1) * UNIT_K]
+                    )
 
-        def load_adj(n):
-            adj_raw[n] = adj_pool.tile([P, NODES], BF16, name="adj_raw")
-            nc.sync.dma_start(out=adj_raw[n][:], in_=adj_tiles[n // 2, n % 2, :, :])
+        def load_scales():
+            for quadrant in range(4):
+                nc.sync.dma_start(
+                    out=w_scales[32 * quadrant : 32 * quadrant + 4, :, :].bitcast(I32),
+                    in_=W1_scales[:, 4 * quadrant : 4 * quadrant + 4, :].rearrange("g r f -> r g f").bitcast(I32),
+                )
 
-        def sort_words(q):
-            ordered[q] = sorted_pool.tile([P, HALF_K], BF16, name="ordered")
-            nc.vector.tensor_copy(
-                out=ordered[q][:].bitcast(F32).rearrange("n (g u p) -> n g u p", g=HALF_GROUPS, u=2),
-                in_=raw[q][:].bitcast(F32).rearrange("n (g p u) -> n g u p", g=HALF_GROUPS, u=2),
+        def load_weights(q):
+            groups = slice(q * UNIT_GROUPS, (q + 1) * UNIT_GROUPS)
+            nc.sync.dma_start(
+                out=w_codes[:, groups, :].bitcast(I32),
+                in_=W1_words[groups].rearrange("g p f t -> p g (f t)").bitcast(I32),
             )
 
-        def transpose_x(q):
-            words = ordered[q][:].bitcast(F32).rearrange("n (g u p) -> n g u p", g=HALF_GROUPS, u=2)
-            grouped[q] = grouped_pool.tile([P, HALF_K], BF16, name="grouped", align_bytes=64)
-            pairs = grouped[q][:].bitcast(F32).rearrange("p (g n u) -> p g n u", g=HALF_GROUPS, u=2)
-            for g0 in range(0, HALF_GROUPS, BANK_GROUPS):
-                bank = banks.tile([P, BANK_GROUPS, 2, P], F32, name="bank")
-                for g in range(BANK_GROUPS):
-                    for u in range(2):
-                        nc.tensor.transpose(bank[:, g, u, :], words[:, g0 + g, u, :], identity[:])
-                nc.scalar.copy(
-                    out=pairs[:, g0 : g0 + BANK_GROUPS, :, :],
-                    in_=bank[:].rearrange("p g u n -> p g n u"),
+        def load_adj(n):
+            adj_raw[n] = adj_raw_pool.tile([P, NODES], BF16, name="adj_raw")
+            nc.sync.dma_start(out=adj_raw[n][:], in_=adj_tiles[n // 2, n % 2, :, :])
+
+        def sort_words(s):
+            ordered[s] = sorted_pool.tile([P, 2, UNIT_K], BF16, name="ordered")
+            for a in range(2):
+                nc.vector.tensor_copy(
+                    out=ordered[s][:, a, :].bitcast(F32).rearrange("n (g u p) -> n g u p", g=UNIT_GROUPS, u=2),
+                    in_=raw[s][:, a, :].bitcast(F32).rearrange("n (g p u) -> n g u p", g=UNIT_GROUPS, u=2),
                 )
 
-        def quantise_x(q):
-            n, h = divmod(q, 2)
-            if h == 0:
-                x_codes[n] = codes_pool.tile([P, K_GROUPS * P], U32, name="x_codes", align_bytes=64)
-                x_scales[n] = codes_pool.tile([P, K_GROUPS * P], U8, name="x_scales", align_bytes=64)
-            for piece in range(2):
-                first = (2 * h + piece) * (HALF_K // 8)
-                cols = slice(first, first + HALF_K // 8)
+        def transpose_x(s):
+            grouped[s] = grouped_pool.tile([P, 2, UNIT_K], BF16, name="grouped", align_bytes=64)
+            for a in range(2):
+                words = ordered[s][:, a, :].bitcast(F32).rearrange("n (g u p) -> n g u p", g=UNIT_GROUPS, u=2)
+                pairs = grouped[s][:, a, :].bitcast(F32).rearrange("p (g n u) -> p g n u", g=UNIT_GROUPS, u=2)
+                for g0 in range(0, UNIT_GROUPS, BANK_GROUPS):
+                    bank = banks.tile([P, BANK_GROUPS, 2, P], F32, name="bank")
+                    for g in range(BANK_GROUPS):
+                        for u in range(2):
+                            nc.tensor.transpose(bank[:, g, u, :], words[:, g0 + g, u, :], identity[:])
+                    nc.scalar.copy(
+                        out=pairs[:, g0 : g0 + BANK_GROUPS, :, :],
+                        in_=bank[:].rearrange("p g u n -> p g n u"),
+                    )
+
+        def quantise_x(s):
+            x_codes[s] = codes_pool.tile([P, 2, UNIT_COLS], U32, name="x_codes", align_bytes=64)
+            x_scales[s] = codes_pool.tile([P, 2, UNIT_COLS], U8, name="x_scales", align_bytes=64)
+            for a in range(2):
                 nc.vector.quantize_mx(
-                    out=x_codes[n][:, cols].bitcast(FP8X4),
-                    scales=x_scales[n][:, cols],
-                    in_=grouped[q][:, piece * (HALF_K // 2) : (piece + 1) * (HALF_K // 2)],
+                    out=x_codes[s][:, a, :].bitcast(FP8X4), scales=x_scales[s][:, a, :], in_=grouped[s][:, a, :]
                 )
 
-        def first_matmul(n, cut):
-            if cut == 0:
-                h_acc[n] = h_banks.tile([P, 512], F32, name="h_acc")
-            cols = slice(FEATURE_CUTS[cut][0], FEATURE_CUTS[cut][1])
-            for g in range(K_GROUPS):
-                nodes = slice(g * P, (g + 1) * P)
-                nc.tensor.matmul_mx(
-                    out=h_acc[n][:, cols],
-                    lhsT=x_codes[n][:, nodes].bitcast(FP8X4),
-                    lhsT_scale=x_scales[n][:, nodes],
-                    rhs=w_codes[:, g, cols].bitcast(FP8X4),
-                    rhs_scale=w_scales[:, g, cols],
-                    start=(g == 0),
-                    stop=(g == K_GROUPS - 1),
-                )
+        def first_matmul(s):
+            for a, (n, q) in enumerate(STEPS[s]):
+                for cut, (first, last) in enumerate(FEATURE_CUTS):
+                    if q == 0:
+                        h_acc[n, cut] = h_banks.tile([P, 512], F32, name="h_acc")
+                    for g in range(UNIT_GROUPS):
+                        k_group = q * UNIT_GROUPS + g
+                        nodes = slice(g * P, (g + 1) * P)
+                        nc.tensor.matmul_mx(
+                            out=h_acc[n, cut][:, 0 : last - first],
+                            lhsT=x_codes[s][:, a, nodes].bitcast(FP8X4),
+                            lhsT_scale=x_scales[s][:, a, nodes],
+                            rhs=w_codes[:, k_group, first:last].bitcast(FP8X4),
+                            rhs_scale=w_scales[:, k_group, first:last],
+                            start=(k_group == 0),
+                            stop=(k_group == K_GROUPS - 1),
+                        )
 
         def transpose_adj(n):
             words = adj_raw[n][:].bitcast(F32).rearrange("i (c u p) -> i c u p", c=NODE_GROUPS, u=2)
@@ -161,9 +188,10 @@ def tile_gcnlayer_pa_k_kernel(tc, x, adj, W1_words, W1_scales, b1, ln_gamma, ln_
                 in_=bank[:].rearrange("p c u i -> p c i u"),
             )
             unused = adj_pool.tile([P, NODES], BF16, name="unused")
-            nc.scalar.activation(out=unused[:], in_=adj_raw[n][:], func=ACT.Copy, accum_out=deg[:, n : n + 1])
-            nc.scalar.activation(out=deg1[:, n : n + 1], in_=deg[:, n : n + 1], func=ACT.Copy, bias=1.0)
-            nc.gpsimd.tensor_tensor(out=dinv[:, n : n + 1], in0=deg1[:, n : n + 1], in1=minus_half[:], op=ALU.pow)
+            nc.scalar.activation(
+                out=unused[:], in_=adj_raw[n][:], func=ACT.Copy, bias=1.0 / NODES, accum_out=deg[:, n : n + 1]
+            )
+            nc.gpsimd.tensor_tensor(out=dinv[:, n : n + 1], in0=deg[:, n : n + 1], in1=minus_half[:], op=ALU.pow)
 
         def quantise_adj(n):
             nc.vector.quantize_mx(
@@ -172,12 +200,21 @@ def tile_gcnlayer_pa_k_kernel(tc, x, adj, W1_words, W1_scales, b1, ln_gamma, ln_
                 in_=adj_grouped[n][:],
             )
 
-        def finish_h(n):
+        def add_bias(n):
+            for cut, (first, last) in enumerate(FEATURE_CUTS):
+                nc.vector.tensor_tensor(
+                    out=hb[:, n, first:last], in0=h_acc[n, cut][:, 0 : last - first], in1=b1_spread[:, first:last],
+                    op=ALU.add,
+                )
+
+        def scale_h(n):
             c, t = divmod(n, TILES_PER_GROUP)
-            nc.vector.tensor_tensor(out=hb[:, n, :], in0=h_acc[n][:, 0:FEAT], in1=b1_spread[:], op=ALU.add)
-            nc.vector.tensor_scalar(
-                out=hs_grouped[:, c, :, t], in0=hb[:, n, :], scalar1=dinv[:, n : n + 1], scalar2=None, op0=ALU.mult
-            )
+            cuts = FEATURE_CUTS if n == TILES - 1 else ((0, FEAT),)
+            for first, last in cuts:
+                nc.vector.tensor_scalar(
+                    out=hs_grouped[:, c, first:last, t], in0=hb[:, n, first:last], scalar1=dinv[:, n : n + 1],
+                    scalar2=None, op0=ALU.mult,
+                )
             if t == TILES_PER_GROUP - 1:
                 values = hs_grouped[:, c, :, :].rearrange("p f t -> p (f t)")
                 for first, last in FEATURE_CUTS:
@@ -198,64 +235,59 @@ def tile_gcnlayer_pa_k_kernel(tc, x, adj, W1_words, W1_scales, b1, ln_gamma, ln_
         for v, vector in enumerate((b1, ln_gamma, ln_beta)):
             nc.scalar.dma_start(out=rows[0:1, v, 0:FEAT], in_=vector.rearrange("(o f) -> o f", o=1))
 
-        load_x(0)
-        load_x(1)
-        load_adj(0)
-        for quadrant in range(4):
-            nc.sync.dma_start(
-                out=w_scales[32 * quadrant : 32 * quadrant + 4, :, :].bitcast(I32),
-                in_=W1_scales[:, 4 * quadrant : 4 * quadrant + 4, :].rearrange("g r f -> r g f").bitcast(I32),
-            )
-        for g0 in range(0, K_GROUPS, 4):
-            nc.sync.dma_start(
-                out=w_codes[:, g0 : g0 + 4, :].bitcast(I32),
-                in_=W1_words[g0 : g0 + 4].rearrange("g p f t -> p g (f t)").bitcast(I32),
-            )
-        load_x(2)
-        load_adj(1)
+        def spread(v, tile):
+            nc.tensor.matmul(out=tile[:], lhsT=ones[:], rhs=rows[:, v, :], start=True, stop=True)
 
-        def sort_and_load_next(q):
-            if q < HALVES:
-                sort_words(q)
-            if q + 3 < HALVES:
-                load_x(q + 3)
+        adj_turn = {min(2 * n + 1, len(STEPS) - 2): n for n in range(TILES)}
 
-        sort_and_load_next(0)
+        def load_turn(s):
+            if s < len(STEPS):
+                load_step(s)
+                if s == 0:
+                    load_scales()
+                if s < QUARTERS:
+                    load_weights(s)
+                if s in adj_turn:
+                    load_adj(adj_turn[s])
+
+        for s in range(RAW_BUFS):
+            load_turn(s)
+        for s in range(2):
+            sort_words(s)
+            load_turn(s + RAW_BUFS)
         transpose_x(0)
-        sort_and_load_next(1)
-        transpose_x(1)
-        transpose_adj(0)
-        bank = banks.tile([P, 512], F32, name="bank")
-        nc.tensor.matmul(out=bank[:], lhsT=ones[:], rhs=rows[:, 0, :], start=True, stop=True)
-        nc.scalar.copy(out=b1_spread[:], in_=bank[:, 0:FEAT])
-        sort_and_load_next(2)
-        quantise_x(0)
-        sort_and_load_next(3)
 
-        for n in range(TILES):
-            more = n + 1 < TILES
-            if more:
-                transpose_x(2 * n + 2)
-            quantise_x(2 * n + 1)
-            quantise_adj(n)
-            if n > 0:
-                finish_h(n - 1)
-            sort_and_load_next(2 * n + 4)
-            first_matmul(n, 0)
-            if more:
-                transpose_x(2 * n + 3)
-                transpose_adj(n + 1)
-                if n + 2 < TILES:
-                    load_adj(n + 2)
-                quantise_x(2 * n + 2)
-            sort_and_load_next(2 * n + 5)
-            first_matmul(n, 1)
-        finish_h(TILES - 1)
-
-        gamma_spread = h_banks.tile([P, 512], F32, name="h_acc")
-        nc.tensor.matmul(out=gamma_spread[:], lhsT=ones[:], rhs=rows[:, 1, :], start=True, stop=True)
-        beta_spread = h_banks.tile([P, 512], F32, name="h_acc")
-        nc.tensor.matmul(out=beta_spread[:], lhsT=ones[:], rhs=rows[:, 2, :], start=True, stop=True)
+        for s in range(len(STEPS)):
+            finished = [n for n in range(TILES) if LAST_STEP[n] == s - 1]
+            if s + 1 < len(STEPS):
+                transpose_x(s + 1)
+            if s in adj_turn:
+                transpose_adj(adj_turn[s])
+            if s == 2:
+                bank = banks.tile([P, 512], F32, name="bank")
+                spread(0, bank)
+                nc.scalar.copy(out=b1_spread[:], in_=bank[:, 0:FEAT])
+            if len(finished) == 2:
+                for n in finished:
+                    add_bias(n)
+            quantise_x(s)
+            if s + 2 < len(STEPS):
+                sort_words(s + 2)
+                load_turn(s + 2 + RAW_BUFS)
+            if len(finished) == 1:
+                add_bias(finished[0])
+            if s in adj_turn:
+                quantise_adj(adj_turn[s])
+            for n in finished:
+                scale_h(n)
+            if s + 1 == len(STEPS):
+                gamma_spread = h_banks.tile([P, 512], F32, name="h_acc")
+                spread(1, gamma_spread)
+                beta_spread = h_banks.tile([P, 512], F32, name="h_acc")
+                spread(2, beta_spread)
+            first_matmul(s)
+        add_bias(TILES - 1)
+        scale_h(TILES - 1)
 
         gelu = {}
         centred = {}

@@ -36,6 +36,7 @@ STEPS = [((0, q), (1, q)) for q in range(QUARTERS)] + [
     ((n, q), (n, q + 1)) for n in range(2, TILES) for q in (0, 2)
 ]
 LAST_STEP = {n: max(s for s, units in enumerate(STEPS) if n in (units[0][0], units[1][0])) for n in range(TILES)}
+ADJ_LEAD = 4
 RAW_BUFS = 5
 
 FLOPS = 2 * NODES * K * FEAT + 2 * NODES * NODES * FEAT
@@ -135,20 +136,20 @@ def tile_gcnlayer_pa_k_kernel(tc, x, adj, W1_words, W1_scales, b1, ln_gamma, ln_
                     in_=raw[s][:, a, :].bitcast(F32).rearrange("n (g p u) -> n g u p", g=UNIT_GROUPS, u=2),
                 )
 
-        def transpose_x(s):
-            grouped[s] = grouped_pool.tile([P, 2, UNIT_K], BF16, name="grouped", align_bytes=64)
-            for a in range(2):
-                words = ordered[s][:, a, :].bitcast(F32).rearrange("n (g u p) -> n g u p", g=UNIT_GROUPS, u=2)
-                pairs = grouped[s][:, a, :].bitcast(F32).rearrange("p (g n u) -> p g n u", g=UNIT_GROUPS, u=2)
-                for g0 in range(0, UNIT_GROUPS, BANK_GROUPS):
-                    bank = banks.tile([P, BANK_GROUPS, 2, P], F32, name="bank")
-                    for g in range(BANK_GROUPS):
-                        for u in range(2):
-                            nc.tensor.transpose(bank[:, g, u, :], words[:, g0 + g, u, :], identity[:])
-                    nc.scalar.copy(
-                        out=pairs[:, g0 : g0 + BANK_GROUPS, :, :],
-                        in_=bank[:].rearrange("p g u n -> p g n u"),
-                    )
+        def transpose_x(s, a):
+            if a == 0:
+                grouped[s] = grouped_pool.tile([P, 2, UNIT_K], BF16, name="grouped", align_bytes=64)
+            words = ordered[s][:, a, :].bitcast(F32).rearrange("n (g u p) -> n g u p", g=UNIT_GROUPS, u=2)
+            pairs = grouped[s][:, a, :].bitcast(F32).rearrange("p (g n u) -> p g n u", g=UNIT_GROUPS, u=2)
+            for g0 in range(0, UNIT_GROUPS, BANK_GROUPS):
+                bank = banks.tile([P, BANK_GROUPS, 2, P], F32, name="bank")
+                for g in range(BANK_GROUPS):
+                    for u in range(2):
+                        nc.tensor.transpose(bank[:, g, u, :], words[:, g0 + g, u, :], identity[:])
+                nc.scalar.copy(
+                    out=pairs[:, g0 : g0 + BANK_GROUPS, :, :],
+                    in_=bank[:].rearrange("p g u n -> p g n u"),
+                )
 
         def quantise_x(s):
             x_codes[s] = codes_pool.tile([P, 2, UNIT_COLS], U32, name="x_codes", align_bytes=64)
@@ -158,23 +159,23 @@ def tile_gcnlayer_pa_k_kernel(tc, x, adj, W1_words, W1_scales, b1, ln_gamma, ln_
                     out=x_codes[s][:, a, :].bitcast(FP8X4), scales=x_scales[s][:, a, :], in_=grouped[s][:, a, :]
                 )
 
-        def first_matmul(s):
-            for a, (n, q) in enumerate(STEPS[s]):
-                for cut, (first, last) in enumerate(FEATURE_CUTS):
-                    if q == 0:
-                        h_acc[n, cut] = h_banks.tile([P, 512], F32, name="h_acc")
-                    for g in range(UNIT_GROUPS):
-                        k_group = q * UNIT_GROUPS + g
-                        nodes = slice(g * P, (g + 1) * P)
-                        nc.tensor.matmul_mx(
-                            out=h_acc[n, cut][:, 0 : last - first],
-                            lhsT=x_codes[s][:, a, nodes].bitcast(FP8X4),
-                            lhsT_scale=x_scales[s][:, a, nodes],
-                            rhs=w_codes[:, k_group, first:last].bitcast(FP8X4),
-                            rhs_scale=w_scales[:, k_group, first:last],
-                            start=(k_group == 0),
-                            stop=(k_group == K_GROUPS - 1),
-                        )
+        def first_matmul(s, a):
+            n, q = STEPS[s][a]
+            for cut, (first, last) in enumerate(FEATURE_CUTS):
+                if q == 0:
+                    h_acc[n, cut] = h_banks.tile([P, 512], F32, name="h_acc")
+                for g in range(UNIT_GROUPS):
+                    k_group = q * UNIT_GROUPS + g
+                    nodes = slice(g * P, (g + 1) * P)
+                    nc.tensor.matmul_mx(
+                        out=h_acc[n, cut][:, 0 : last - first],
+                        lhsT=x_codes[s][:, a, nodes].bitcast(FP8X4),
+                        lhsT_scale=x_scales[s][:, a, nodes],
+                        rhs=w_codes[:, k_group, first:last].bitcast(FP8X4),
+                        rhs_scale=w_scales[:, k_group, first:last],
+                        start=(k_group == 0),
+                        stop=(k_group == K_GROUPS - 1),
+                    )
 
         def transpose_adj(n):
             words = adj_raw[n][:].bitcast(F32).rearrange("i (c u p) -> i c u p", c=NODE_GROUPS, u=2)
@@ -232,60 +233,64 @@ def tile_gcnlayer_pa_k_kernel(tc, x, adj, W1_words, W1_scales, b1, ln_gamma, ln_
         nc.vector.memset(minus_half[:], -0.5)
         make_identity(nc, identity[:])
 
-        for v, vector in enumerate((b1, ln_gamma, ln_beta)):
-            nc.scalar.dma_start(out=rows[0:1, v, 0:FEAT], in_=vector.rearrange("(o f) -> o f", o=1))
-
         def spread(v, tile):
             nc.tensor.matmul(out=tile[:], lhsT=ones[:], rhs=rows[:, v, :], start=True, stop=True)
 
-        adj_turn = {min(2 * n + 1, len(STEPS) - 2): n for n in range(TILES)}
+        steps = len(STEPS)
+        adj_turn = {4 + n + n // 2: n for n in range(TILES)}
+        scale_turn = {n: max(LAST_STEP[n] + 1, turn + 2) for turn, n in adj_turn.items()}
 
         def load_turn(s):
-            if s < len(STEPS):
+            if s < steps:
                 load_step(s)
-                if s == 0:
-                    load_scales()
                 if s < QUARTERS:
                     load_weights(s)
-                if s in adj_turn:
-                    load_adj(adj_turn[s])
+                if s == 0:
+                    load_scales()
+                if s == 1:
+                    for v, vector in enumerate((b1, ln_gamma, ln_beta)):
+                        nc.sync.dma_start(out=rows[0:1, v, 0:FEAT], in_=vector.rearrange("(o f) -> o f", o=1))
 
         for s in range(RAW_BUFS):
             load_turn(s)
         for s in range(2):
             sort_words(s)
             load_turn(s + RAW_BUFS)
-        transpose_x(0)
+            if s == 0:
+                for a in range(2):
+                    transpose_x(0, a)
 
-        for s in range(len(STEPS)):
+        for s in range(steps):
             finished = [n for n in range(TILES) if LAST_STEP[n] == s - 1]
-            if s + 1 < len(STEPS):
-                transpose_x(s + 1)
+            if s + 1 < steps:
+                for a in range(2):
+                    transpose_x(s + 1, a)
+            quantise_x(s)
+            if s + 1 == steps:
+                gamma_spread = h_banks.tile([P, 512], F32, name="h_acc")
+                spread(1, gamma_spread)
+                beta_spread = h_banks.tile([P, 512], F32, name="h_acc")
+                spread(2, beta_spread)
+            for n in finished:
+                add_bias(n)
+            first_matmul(s, 0)
             if s in adj_turn:
                 transpose_adj(adj_turn[s])
             if s == 2:
                 bank = banks.tile([P, 512], F32, name="bank")
                 spread(0, bank)
                 nc.scalar.copy(out=b1_spread[:], in_=bank[:, 0:FEAT])
-            if len(finished) == 2:
-                for n in finished:
-                    add_bias(n)
-            quantise_x(s)
-            if s + 2 < len(STEPS):
+            if s + 2 < steps:
                 sort_words(s + 2)
                 load_turn(s + 2 + RAW_BUFS)
-            if len(finished) == 1:
-                add_bias(finished[0])
-            if s in adj_turn:
-                quantise_adj(adj_turn[s])
-            for n in finished:
-                scale_h(n)
-            if s + 1 == len(STEPS):
-                gamma_spread = h_banks.tile([P, 512], F32, name="h_acc")
-                spread(1, gamma_spread)
-                beta_spread = h_banks.tile([P, 512], F32, name="h_acc")
-                spread(2, beta_spread)
-            first_matmul(s)
+            if s + ADJ_LEAD in adj_turn:
+                load_adj(adj_turn[s + ADJ_LEAD])
+            if s - 1 in adj_turn:
+                quantise_adj(adj_turn[s - 1])
+            for n in range(TILES - 1):
+                if scale_turn[n] == s:
+                    scale_h(n)
+            first_matmul(s, 1)
         add_bias(TILES - 1)
         scale_h(TILES - 1)
 

@@ -132,8 +132,8 @@ def tile_gcnlayer_pa_k_kernel(tc, x, adj, W1_words, W1_scales, b1, ln_gamma, ln_
             ordered[s] = sorted_pool.tile([P, 2, UNIT_K], BF16, name="ordered")
             for a in range(2):
                 nc.vector.tensor_copy(
-                    out=ordered[s][:, a, :].bitcast(F32).rearrange("n (g u p) -> n g u p", g=UNIT_GROUPS, u=2),
-                    in_=raw[s][:, a, :].bitcast(F32).rearrange("n (g p u) -> n g u p", g=UNIT_GROUPS, u=2),
+                    out=ordered[s][:, a, :].bitcast(F32).rearrange("n (g u p) -> n g p u", g=UNIT_GROUPS, u=2),
+                    in_=raw[s][:, a, :].bitcast(F32).rearrange("n (g p u) -> n g p u", g=UNIT_GROUPS, u=2),
                 )
 
         def transpose_x(s, a):

@@ -36,8 +36,8 @@ STEPS = [((0, q), (1, q)) for q in range(QUARTERS)] + [
     ((n, q), (n, q + 1)) for n in range(2, TILES) for q in (0, 2)
 ]
 LAST_STEP = {n: max(s for s, units in enumerate(STEPS) if n in (units[0][0], units[1][0])) for n in range(TILES)}
-ADJ_LEAD = 4
-RAW_BUFS = 5
+SINGLE_TURNS = 8
+RAW_BUFS = 4
 
 FLOPS = 2 * NODES * K * FEAT + 2 * NODES * NODES * FEAT
 
@@ -56,19 +56,21 @@ def tile_gcnlayer_pa_k_kernel(tc, x, adj, W1_words, W1_scales, b1, ln_gamma, ln_
         ctx.enter_context(tc.manual_schedule())
         keep = ctx.enter_context(tc.tile_pool(name="keep", bufs=1))
         raw_pool = ctx.enter_context(tc.tile_pool(name="raw", bufs=RAW_BUFS))
-        sorted_pool = ctx.enter_context(tc.tile_pool(name="sorted", bufs=3))
+        sorted_pool = ctx.enter_context(tc.tile_pool(name="sorted", bufs=4))
         grouped_pool = ctx.enter_context(tc.tile_pool(name="grouped", bufs=3))
-        codes_pool = ctx.enter_context(tc.tile_pool(name="codes", bufs=3))
+        codes_pool = ctx.enter_context(tc.tile_pool(name="codes", bufs=4))
         adj_raw_pool = ctx.enter_context(tc.tile_pool(name="adj_raw", bufs=4))
         adj_pool = ctx.enter_context(tc.tile_pool(name="adj", bufs=2))
         tail_pool = ctx.enter_context(tc.tile_pool(name="tail", bufs=4))
+        h_banks = ctx.enter_context(tc.psum_pool(name="h_banks", bufs=2))
         banks = ctx.enter_context(tc.psum_pool(name="banks", bufs=4))
-        h_banks = ctx.enter_context(tc.psum_pool(name="h_banks", bufs=4))
+        narrow_banks = ctx.enter_context(tc.psum_pool(name="narrow_banks", bufs=2))
 
         identity = keep.tile([P, P], F32)
         ones = keep.tile([P, P], BF16)
         rows = keep.tile([P, 3, 512], BF16)
         b1_spread = keep.tile([P, FEAT], F32)
+        scaled_b1 = keep.tile([P, FEAT], F32)
         minus_half = keep.tile([P, 1], F32)
         warm = keep.tile([P, 1], F32)
         w_codes = keep.tile([P, K_GROUPS, FEAT], U32, align_bytes=64)
@@ -95,6 +97,8 @@ def tile_gcnlayer_pa_k_kernel(tc, x, adj, W1_words, W1_scales, b1, ln_gamma, ln_
         adj_raw = {}
         adj_grouped = {}
         h_acc = {}
+        filled = []
+        narrow_free = []
 
         def load_step(s):
             raw[s] = raw_pool.tile([P, 2, UNIT_K], BF16, name="raw")
@@ -136,13 +140,22 @@ def tile_gcnlayer_pa_k_kernel(tc, x, adj, W1_words, W1_scales, b1, ln_gamma, ln_
                     in_=raw[s][:, a, :].bitcast(F32).rearrange("n (g p u) -> n g p u", g=UNIT_GROUPS, u=2),
                 )
 
+        def next_bank():
+            turn = len(filled) % 6 if narrow_free else len(filled) % 4
+            filled.append(turn)
+            if turn < 4:
+                bank = banks.tile([P, BANK_GROUPS, 2, P], F32, name="bank")
+            else:
+                bank = narrow_banks.tile([P, BANK_GROUPS, 2, P], F32, name="narrow")
+            return bank
+
         def transpose_x(s, a):
             if a == 0:
                 grouped[s] = grouped_pool.tile([P, 2, UNIT_K], BF16, name="grouped", align_bytes=64)
             words = ordered[s][:, a, :].bitcast(F32).rearrange("n (g u p) -> n g u p", g=UNIT_GROUPS, u=2)
             pairs = grouped[s][:, a, :].bitcast(F32).rearrange("p (g n u) -> p g n u", g=UNIT_GROUPS, u=2)
             for g0 in range(0, UNIT_GROUPS, BANK_GROUPS):
-                bank = banks.tile([P, BANK_GROUPS, 2, P], F32, name="bank")
+                bank = next_bank()
                 for g in range(BANK_GROUPS):
                     for u in range(2):
                         nc.tensor.transpose(bank[:, g, u, :], words[:, g0 + g, u, :], identity[:])
@@ -159,16 +172,20 @@ def tile_gcnlayer_pa_k_kernel(tc, x, adj, W1_words, W1_scales, b1, ln_gamma, ln_
                     out=x_codes[s][:, a, :].bitcast(FP8X4), scales=x_scales[s][:, a, :], in_=grouped[s][:, a, :]
                 )
 
-        def first_matmul(s, a):
-            n, q = STEPS[s][a]
-            for cut, (first, last) in enumerate(FEATURE_CUTS):
-                if q == 0:
+        def first_matmul(s, cut):
+            first, last = FEATURE_CUTS[cut]
+            for a, (n, q) in enumerate(STEPS[s]):
+                if q == 0 and (cut == 0 or n == TILES - 1):
                     h_acc[n, cut] = h_banks.tile([P, 512], F32, name="h_acc")
+                elif q == 0 and s == 0:
+                    h_acc[n, cut] = narrow_banks.tile([P, 512], F32, name="narrow")
+                elif q == 0:
+                    h_acc[n, cut] = h_acc[n, 0]
                 for g in range(UNIT_GROUPS):
                     k_group = q * UNIT_GROUPS + g
                     nodes = slice(g * P, (g + 1) * P)
                     nc.tensor.matmul_mx(
-                        out=h_acc[n, cut][:, 0 : last - first],
+                        out=h_acc[n, cut][:, first:last],
                         lhsT=x_codes[s][:, a, nodes].bitcast(FP8X4),
                         lhsT_scale=x_scales[s][:, a, nodes],
                         rhs=w_codes[:, k_group, first:last].bitcast(FP8X4),
@@ -179,7 +196,7 @@ def tile_gcnlayer_pa_k_kernel(tc, x, adj, W1_words, W1_scales, b1, ln_gamma, ln_
 
         def transpose_adj(n):
             words = adj_raw[n][:].bitcast(F32).rearrange("i (c u p) -> i c u p", c=NODE_GROUPS, u=2)
-            bank = banks.tile([P, NODE_GROUPS, 2, P], F32, name="bank")
+            bank = next_bank()
             for c in range(NODE_GROUPS):
                 for u in range(2):
                     nc.tensor.transpose(bank[:, c, u, :], words[:, c, u, :], identity[:])
@@ -188,6 +205,8 @@ def tile_gcnlayer_pa_k_kernel(tc, x, adj, W1_words, W1_scales, b1, ln_gamma, ln_
                 out=adj_grouped[n][:].bitcast(F32).rearrange("p (c i u) -> p c i u", c=NODE_GROUPS, u=2),
                 in_=bank[:].rearrange("p c u i -> p c i u"),
             )
+
+        def degree(n):
             unused = adj_pool.tile([P, NODES], BF16, name="unused")
             nc.scalar.activation(
                 out=unused[:], in_=adj_raw[n][:], func=ACT.Copy, bias=1.0 / NODES, accum_out=deg[:, n : n + 1]
@@ -202,28 +221,34 @@ def tile_gcnlayer_pa_k_kernel(tc, x, adj, W1_words, W1_scales, b1, ln_gamma, ln_
             )
 
         def add_bias(n):
-            for cut, (first, last) in enumerate(FEATURE_CUTS):
+            split = FEATURE_CUTS if n < 2 or n == TILES - 1 else ((0, FEAT),)
+            for cut, (first, last) in enumerate(split):
                 nc.vector.tensor_tensor(
-                    out=hb[:, n, first:last], in0=h_acc[n, cut][:, 0 : last - first], in1=b1_spread[:, first:last],
+                    out=hb[:, n, first:last], in0=h_acc[n, cut][:, first:last], in1=b1_spread[:, first:last],
                     op=ALU.add,
                 )
 
-        def scale_h(n):
+        def scale_h(n, first, last):
             c, t = divmod(n, TILES_PER_GROUP)
-            cuts = FEATURE_CUTS if n == TILES - 1 else ((0, FEAT),)
-            for first, last in cuts:
-                nc.vector.tensor_scalar(
-                    out=hs_grouped[:, c, first:last, t], in0=hb[:, n, first:last], scalar1=dinv[:, n : n + 1],
-                    scalar2=None, op0=ALU.mult,
-                )
-            if t == TILES_PER_GROUP - 1:
-                values = hs_grouped[:, c, :, :].rearrange("p f t -> p (f t)")
-                for first, last in FEATURE_CUTS:
-                    nc.vector.quantize_mx(
-                        out=hs_codes[:, c, first:last].bitcast(FP8X4),
-                        scales=hs_scales[:, c, first:last],
-                        in_=values[:, first * PACK : last * PACK],
-                    )
+            nc.vector.tensor_scalar(
+                out=hs_grouped[:, c, first:last, t], in0=hb[:, n, first:last], scalar1=dinv[:, n : n + 1],
+                scalar2=None, op0=ALU.mult,
+            )
+
+        def last_hs(cut):
+            n = TILES - 1
+            first, last = FEATURE_CUTS[cut]
+            nc.vector.scalar_tensor_tensor(
+                out=hs_grouped[:, NODE_GROUPS - 1, first:last, PACK - 1], in0=h_acc[n, cut][:, first:last],
+                scalar=dinv[:, n : n + 1], in1=scaled_b1[:, first:last], op0=ALU.mult, op1=ALU.add,
+            )
+
+        def quantise_hs(c, first, last):
+            nc.vector.quantize_mx(
+                out=hs_codes[:, c, first:last].bitcast(FP8X4),
+                scales=hs_scales[:, c, first:last],
+                in_=hs_grouped[:, c, first:last, :].rearrange("p f t -> p (f t)"),
+            )
 
         nc.vector.memset(warm[:], 0.0)
         nc.scalar.activation(out=warm[:], in_=warm[:], func=ACT.Gelu)
@@ -237,8 +262,6 @@ def tile_gcnlayer_pa_k_kernel(tc, x, adj, W1_words, W1_scales, b1, ln_gamma, ln_
             nc.tensor.matmul(out=tile[:], lhsT=ones[:], rhs=rows[:, v, :], start=True, stop=True)
 
         steps = len(STEPS)
-        adj_turn = {4 + n + n // 2: n for n in range(TILES)}
-        scale_turn = {n: max(LAST_STEP[n] + 1, turn + 2) for turn, n in adj_turn.items()}
 
         def load_turn(s):
             if s < steps:
@@ -251,81 +274,129 @@ def tile_gcnlayer_pa_k_kernel(tc, x, adj, W1_words, W1_scales, b1, ln_gamma, ln_
                     for v, vector in enumerate((b1, ln_gamma, ln_beta)):
                         nc.sync.dma_start(out=rows[0:1, v, 0:FEAT], in_=vector.rearrange("(o f) -> o f", o=1))
 
+        turns = [(s,) for s in range(SINGLE_TURNS)] + [(s, s + 1) for s in range(SINGLE_TURNS, steps, 2)]
+        adj_of = {len(turns) - TILES + n: n for n in range(TILES)}
         for s in range(RAW_BUFS):
             load_turn(s)
+        loaded = RAW_BUFS
         for s in range(2):
             sort_words(s)
-            load_turn(s + RAW_BUFS)
+            load_turn(loaded)
+            loaded += 1
             if s == 0:
                 for a in range(2):
                     transpose_x(0, a)
+        sorted_to = 2
+        transposed_to = 1
 
-        for s in range(steps):
-            finished = [n for n in range(TILES) if LAST_STEP[n] == s - 1]
-            if s + 1 < steps:
+        for i, turn in enumerate(turns):
+            for s in range(transposed_to, min(turn[-1] + 2, steps)):
                 for a in range(2):
-                    transpose_x(s + 1, a)
-            quantise_x(s)
-            if s + 1 == steps:
-                gamma_spread = h_banks.tile([P, 512], F32, name="h_acc")
-                spread(1, gamma_spread)
-                beta_spread = h_banks.tile([P, 512], F32, name="h_acc")
-                spread(2, beta_spread)
-            for n in finished:
-                add_bias(n)
-            first_matmul(s, 0)
-            if s in adj_turn:
-                transpose_adj(adj_turn[s])
-            if s == 2:
+                    transpose_x(s, a)
+            transposed_to = turn[-1] + 2
+            if i in adj_of:
+                transpose_adj(adj_of[i])
+                for n in {TILES - 2: (TILES - 2, TILES - 1), TILES - 1: ()}.get(adj_of[i], (adj_of[i],)):
+                    degree(n)
+            if i == 2:
                 bank = banks.tile([P, 512], F32, name="bank")
+                filled.append(0)
                 spread(0, bank)
                 nc.scalar.copy(out=b1_spread[:], in_=bank[:, 0:FEAT])
-            if s + 2 < steps:
-                sort_words(s + 2)
-                load_turn(s + 2 + RAW_BUFS)
-            if s + ADJ_LEAD in adj_turn:
-                load_adj(adj_turn[s + ADJ_LEAD])
-            if s - 1 in adj_turn:
-                quantise_adj(adj_turn[s - 1])
-            for n in range(TILES - 1):
-                if scale_turn[n] == s:
-                    scale_h(n)
-            first_matmul(s, 1)
+            finished = [n for n in range(TILES) if LAST_STEP[n] in range(turns[i - 1][0], turn[0])] if i else []
+            scale_now = [i - 5] if 0 <= i - 5 < TILES - 1 else []
+            next_steps = turns[min(i + 1, len(turns) - 1)]
+            sort_now = list(range(sorted_to, min(next_steps[-1] + 2, steps)))
+            for j in range(2):
+                if j < len(turn):
+                    quantise_x(turn[j])
+                for n in finished if j == 0 else ():
+                    add_bias(n)
+                    if n == 1:
+                        narrow_free.append(True)
+                for s in sort_now[j : j + 1]:
+                    sort_words(s)
+                    sorted_to = s + 1
+                    load_turn(loaded)
+                    loaded += 1
+            if i + 4 in adj_of:
+                load_adj(adj_of[i + 4])
+            if i - 1 in adj_of:
+                quantise_adj(adj_of[i - 1])
+            if i + 1 == len(turns):
+                quantise_adj(TILES - 1)
+            for n in scale_now:
+                scale_h(n, 0, FEAT)
+                if n == TILES_PER_GROUP - 1:
+                    for first, last in FEATURE_CUTS:
+                        quantise_hs(0, first, last)
+            if i + 1 == len(turns):
+                n = TILES - 1
+                nc.scalar.activation(out=scaled_b1[:], in_=b1_spread[:], func=ACT.Copy, scale=dinv[:, n : n + 1])
+            for s in turn:
+                first_matmul(s, 0)
+                if s < QUARTERS:
+                    first_matmul(s, 1)
+            if turn[-1] >= QUARTERS and turn[-1] % 2 == 1:
+                first_matmul(turn[-1] - 1, 1)
+                first_matmul(turn[-1], 1)
+        gamma_spread = narrow_banks.tile([P, 512], F32, name="narrow")
+        spread(1, gamma_spread)
+        beta_spread = narrow_banks.tile([P, 512], F32, name="narrow")
+        spread(2, beta_spread)
+        for cut, (first, last) in enumerate(FEATURE_CUTS):
+            last_hs(cut)
+            quantise_hs(NODE_GROUPS - 1, first, last)
         add_bias(TILES - 1)
-        scale_h(TILES - 1)
 
         gelu = {}
         centred = {}
+        summed = {}
+        aggs = {}
 
-        def second_matmul(i):
-            one = slice(i, i + 1)
-            agg = banks.tile([P, 512], F32, name="bank")
-            for first, last in FEATURE_CUTS:
-                cols = slice(first, last)
-                for c in range(NODE_GROUPS):
-                    nc.tensor.matmul_mx(
-                        out=agg[:, cols],
-                        lhsT=adj_codes[:, i, c, :].bitcast(FP8X4),
-                        lhsT_scale=adj_scales[:, i, c, :],
-                        rhs=hs_codes[:, c, cols].bitcast(FP8X4),
-                        rhs_scale=hs_scales[:, c, cols],
-                        start=(c == 0),
-                        stop=(c == NODE_GROUPS - 1),
-                    )
-            summed = tail_pool.tile([P, FEAT], F32, name="summed")
+        def multiply_adj(i, cut):
+            if cut == 0:
+                aggs[i] = banks.tile([P, 512], F32, name="bank")
+            cols = slice(FEATURE_CUTS[cut][0], FEATURE_CUTS[cut][1])
+            for c in range(NODE_GROUPS):
+                nc.tensor.matmul_mx(
+                    out=aggs[i][:, cols],
+                    lhsT=adj_codes[:, i, c, :].bitcast(FP8X4),
+                    lhsT_scale=adj_scales[:, i, c, :],
+                    rhs=hs_codes[:, c, cols].bitcast(FP8X4),
+                    rhs_scale=hs_scales[:, c, cols],
+                    start=(c == 0),
+                    stop=(c == NODE_GROUPS - 1),
+                )
+
+        def add_hs(i):
+            summed[i] = tail_pool.tile([P, FEAT], F32, name="summed")
             nc.vector.scalar_tensor_tensor(
-                out=summed[:], in0=hb[:, i, :], scalar=dinv[:, one], in1=agg[:, 0:FEAT], op0=ALU.mult, op1=ALU.add
+                out=summed[i][:], in0=hb[:, i, :], scalar=dinv[:, i : i + 1], in1=aggs[i][:, 0:FEAT],
+                op0=ALU.mult, op1=ALU.add,
             )
+
+        def activate(i):
+            one = slice(i, i + 1)
             gelu[i] = tail_pool.tile([P, FEAT], F32, name="gelu")
             nc.scalar.activation(
-                out=gelu[i][:], in_=summed[:], func=ACT.Gelu, scale=dinv[:, one], accum_out=g_sum[:, one]
+                out=gelu[i][:], in_=summed[i][:], func=ACT.Gelu, scale=dinv[:, one], accum_out=g_sum[:, one]
             )
+
+        def mean(i):
+            one = slice(i, i + 1)
             nc.scalar.activation(out=minus_mean[:, one], in_=g_sum[:, one], func=ACT.Copy, scale=-1.0 / FEAT)
-            squares = tail_pool.tile([P, FEAT], F32, name="squares")
+
+        def square(i):
+            one = slice(i, i + 1)
+            squares = tail_pool.tile([P, FEAT], F32, name="squares", bufs=1)
             nc.scalar.activation(
                 out=squares[:], in_=gelu[i][:], func=ACT.Square, bias=minus_mean[:, one], scale=1.0,
                 accum_out=sq_sum[:, one],
             )
+
+        def deviation(i):
+            one = slice(i, i + 1)
             nc.scalar.activation(out=var_eps[:, one], in_=sq_sum[:, one], func=ACT.Copy, scale=1.0 / FEAT, bias=EPS)
             nc.gpsimd.tensor_tensor(out=rstd[:, one], in0=var_eps[:, one], in1=minus_half[:], op=ALU.pow)
 
@@ -344,10 +415,25 @@ def tile_gcnlayer_pa_k_kernel(tc, x, adj, W1_words, W1_scales, b1, ln_gamma, ln_
             )
             nc.sync.dma_start(out=out_tiles[i // 2, i % 2, :, :], in_=result[:])
 
+        for cut in range(2):
+            for i in range(4):
+                multiply_adj(i, cut)
+        for i in range(2):
+            add_hs(i)
         for step in range(TILES + 2):
+            if step + 2 < TILES:
+                if step + 2 >= 4:
+                    for cut in range(2):
+                        multiply_adj(step + 2, cut)
+                add_hs(step + 2)
             if step < TILES:
-                second_matmul(step)
+                activate(step)
             if 0 <= step - 1 < TILES:
+                square(step - 1)
+            if step < TILES:
+                mean(step)
+            if 0 <= step - 1 < TILES:
+                deviation(step - 1)
                 centre(step - 1)
-            if 0 <= step - 2:
+            if 0 <= step - 2 < TILES:
                 scale_and_store(step - 2)

@@ -208,9 +208,15 @@ def tile_gcnlayer_pa_k_kernel(tc, x, adj, W1_words, W1_scales, b1, ln_gamma, ln_
 
         def degree(n):
             unused = adj_pool.tile([P, NODES], BF16, name="unused")
-            nc.scalar.activation(
-                out=unused[:], in_=adj_raw[n][:], func=ACT.Copy, bias=1.0 / NODES, accum_out=deg[:, n : n + 1]
-            )
+            if n < TILES - 1:
+                nc.scalar.activation(
+                    out=unused[:], in_=adj_raw[n][:], func=ACT.Copy, bias=1.0 / NODES, accum_out=deg[:, n : n + 1]
+                )
+            else:
+                nc.vector.tensor_scalar(
+                    out=unused[:], in0=adj_raw[n][:], scalar1=1.0, scalar2=1.0, op0=ALU.mult, op1=ALU.add,
+                    accum_out=deg[:, n : n + 1],
+                )
             nc.gpsimd.tensor_tensor(out=dinv[:, n : n + 1], in0=deg[:, n : n + 1], in1=minus_half[:], op=ALU.pow)
 
         def quantise_adj(n):
@@ -296,8 +302,8 @@ def tile_gcnlayer_pa_k_kernel(tc, x, adj, W1_words, W1_scales, b1, ln_gamma, ln_
             transposed_to = turn[-1] + 2
             if i in adj_of:
                 transpose_adj(adj_of[i])
-                for n in {TILES - 2: (TILES - 2, TILES - 1), TILES - 1: ()}.get(adj_of[i], (adj_of[i],)):
-                    degree(n)
+                if adj_of[i] < TILES - 1:
+                    degree(adj_of[i])
             if i == 2:
                 bank = banks.tile([P, 512], F32, name="bank")
                 filled.append(0)
@@ -314,6 +320,8 @@ def tile_gcnlayer_pa_k_kernel(tc, x, adj, W1_words, W1_scales, b1, ln_gamma, ln_
                     add_bias(n)
                     if n == 1:
                         narrow_free.append(True)
+                if j == 0 and i + 1 == len(turns):
+                    degree(TILES - 1)
                 for s in sort_now[j : j + 1]:
                     sort_words(s)
                     sorted_to = s + 1
@@ -337,7 +345,9 @@ def tile_gcnlayer_pa_k_kernel(tc, x, adj, W1_words, W1_scales, b1, ln_gamma, ln_
                 first_matmul(s, 0)
                 if s < QUARTERS:
                     first_matmul(s, 1)
-            if turn[-1] >= QUARTERS and turn[-1] % 2 == 1:
+                if i + 1 == len(turns):
+                    first_matmul(s, 1)
+            if turn[-1] >= QUARTERS and turn[-1] % 2 == 1 and i + 1 < len(turns):
                 first_matmul(turn[-1] - 1, 1)
                 first_matmul(turn[-1], 1)
         gamma_spread = narrow_banks.tile([P, 512], F32, name="narrow")
@@ -408,7 +418,7 @@ def tile_gcnlayer_pa_k_kernel(tc, x, adj, W1_words, W1_scales, b1, ln_gamma, ln_
             )
 
         def scale_and_store(i):
-            result = tail_pool.tile([P, FEAT], F32, name="result")
+            result = tail_pool.tile([P, FEAT], F32, name="result", bufs=6)
             nc.vector.scalar_tensor_tensor(
                 out=result[:], in0=centred[i][:], scalar=rstd[:, i : i + 1], in1=beta_spread[:, 0:FEAT],
                 op0=ALU.mult, op1=ALU.add,

@@ -36,7 +36,7 @@ STEPS = [((0, q), (1, q)) for q in range(QUARTERS)] + [
     ((n, q), (n, q + 1)) for n in range(2, TILES) for q in (0, 2)
 ]
 LAST_STEP = {n: max(s for s, units in enumerate(STEPS) if n in (units[0][0], units[1][0])) for n in range(TILES)}
-SINGLE_TURNS = 8
+SINGLE_TURNS = 6
 RAW_BUFS = 4
 
 FLOPS = 2 * NODES * K * FEAT + 2 * NODES * NODES * FEAT
@@ -268,20 +268,23 @@ def tile_gcnlayer_pa_k_kernel(tc, x, adj, W1_words, W1_scales, b1, ln_gamma, ln_
             nc.tensor.matmul(out=tile[:], lhsT=ones[:], rhs=rows[:, v, :], start=True, stop=True)
 
         steps = len(STEPS)
+        turns = [(s,) for s in range(SINGLE_TURNS)] + [(s, s + 1) for s in range(SINGLE_TURNS, steps, 2)]
+        adj_of = {len(turns) - TILES + n: n for n in range(TILES)}
 
         def load_turn(s):
             if s < steps:
                 load_step(s)
-                if s < QUARTERS:
-                    load_weights(s)
-                if s == 0:
+                if 0 < s <= QUARTERS:
+                    load_weights(s - 1)
+                if s == 1:
                     load_scales()
+                for i, n in adj_of.items():
+                    if s == min(turns[i][-1] + 1, steps - 1):
+                        load_adj(n)
                 if s == 1:
                     for v, vector in enumerate((b1, ln_gamma, ln_beta)):
                         nc.sync.dma_start(out=rows[0:1, v, 0:FEAT], in_=vector.rearrange("(o f) -> o f", o=1))
 
-        turns = [(s,) for s in range(SINGLE_TURNS)] + [(s, s + 1) for s in range(SINGLE_TURNS, steps, 2)]
-        adj_of = {len(turns) - TILES + n: n for n in range(TILES)}
         for s in range(RAW_BUFS):
             load_turn(s)
         loaded = RAW_BUFS
@@ -310,7 +313,7 @@ def tile_gcnlayer_pa_k_kernel(tc, x, adj, W1_words, W1_scales, b1, ln_gamma, ln_
                 spread(0, bank)
                 nc.scalar.copy(out=b1_spread[:], in_=bank[:, 0:FEAT])
             finished = [n for n in range(TILES) if LAST_STEP[n] in range(turns[i - 1][0], turn[0])] if i else []
-            scale_now = [i - 5] if 0 <= i - 5 < TILES - 1 else []
+            scale_now = [i - 4] if 0 <= i - 4 < TILES - 1 else []
             next_steps = turns[min(i + 1, len(turns) - 1)]
             sort_now = list(range(sorted_to, min(next_steps[-1] + 2, steps)))
             for j in range(2):
@@ -327,8 +330,6 @@ def tile_gcnlayer_pa_k_kernel(tc, x, adj, W1_words, W1_scales, b1, ln_gamma, ln_
                     sorted_to = s + 1
                     load_turn(loaded)
                     loaded += 1
-            if i + 4 in adj_of:
-                load_adj(adj_of[i + 4])
             if i - 1 in adj_of:
                 quantise_adj(adj_of[i - 1])
             if i + 1 == len(turns):

@@ -103,7 +103,7 @@ def tile_gcnlayer_pa_k_kernel(tc, x, adj, W1_words, W1_scales, b1, ln_gamma, ln_
         def load_step(s):
             raw[s] = raw_pool.tile([P, 2, UNIT_K], BF16, name="raw")
             (n0, q0), (n1, q1) = STEPS[s]
-            if n0 == n1:
+            if n0 == n1 and s > QUARTERS + 1:
                 nc.sync.dma_start(
                     out=raw[s][:].rearrange("n a k -> n (a k)"),
                     in_=x_tiles[n0 // 2, n0 % 2, :, q0 * UNIT_K : (q1 + 1) * UNIT_K],
@@ -263,6 +263,8 @@ def tile_gcnlayer_pa_k_kernel(tc, x, adj, W1_words, W1_scales, b1, ln_gamma, ln_
         nc.vector.memset(ones[:], 1.0)
         nc.vector.memset(minus_half[:], -0.5)
         make_identity(nc, identity[:])
+        for v, vector in enumerate((b1, ln_gamma, ln_beta)):
+            nc.gpsimd.dma_start(out=rows[0:1, v, 0:FEAT], in_=vector.rearrange("(o f) -> o f", o=1))
 
         def spread(v, tile):
             nc.tensor.matmul(out=tile[:], lhsT=ones[:], rhs=rows[:, v, :], start=True, stop=True)
@@ -274,16 +276,13 @@ def tile_gcnlayer_pa_k_kernel(tc, x, adj, W1_words, W1_scales, b1, ln_gamma, ln_
         def load_turn(s):
             if s < steps:
                 load_step(s)
+                if s == 0:
+                    load_scales()
                 if 0 < s <= QUARTERS:
                     load_weights(s - 1)
-                if s == 1:
-                    load_scales()
                 for i, n in adj_of.items():
                     if s == min(turns[i][-1] + 1, steps - 1):
                         load_adj(n)
-                if s == 1:
-                    for v, vector in enumerate((b1, ln_gamma, ln_beta)):
-                        nc.sync.dma_start(out=rows[0:1, v, 0:FEAT], in_=vector.rearrange("(o f) -> o f", o=1))
 
         for s in range(RAW_BUFS):
             load_turn(s)

@@ -36,7 +36,7 @@ STEPS = [((0, q), (1, q)) for q in range(QUARTERS)] + [
     ((n, q), (n, q + 1)) for n in range(2, TILES) for q in (0, 2)
 ]
 LAST_STEP = {n: max(s for s, units in enumerate(STEPS) if n in (units[0][0], units[1][0])) for n in range(TILES)}
-SINGLE_TURNS = 6
+SINGLE_TURNS = 8
 RAW_BUFS = 4
 
 FLOPS = 2 * NODES * K * FEAT + 2 * NODES * NODES * FEAT
@@ -114,11 +114,13 @@ def tile_gcnlayer_pa_k_kernel(tc, x, adj, W1_words, W1_scales, b1, ln_gamma, ln_
                         out=raw[s][:, a, :], in_=x_tiles[n // 2, n % 2, :, q * UNIT_K : (q + 1) * UNIT_K]
                     )
 
-        def load_scales():
+        def load_scales(first, last):
             for quadrant in range(4):
                 nc.sync.dma_start(
-                    out=w_scales[32 * quadrant : 32 * quadrant + 4, :, :].bitcast(I32),
-                    in_=W1_scales[:, 4 * quadrant : 4 * quadrant + 4, :].rearrange("g r f -> r g f").bitcast(I32),
+                    out=w_scales[32 * quadrant : 32 * quadrant + 4, first:last, :].bitcast(I32),
+                    in_=W1_scales[first:last, 4 * quadrant : 4 * quadrant + 4, :]
+                    .rearrange("g r f -> r g f")
+                    .bitcast(I32),
                 )
 
         def load_weights(q):
@@ -258,7 +260,8 @@ def tile_gcnlayer_pa_k_kernel(tc, x, adj, W1_words, W1_scales, b1, ln_gamma, ln_
 
         nc.vector.memset(warm[:], 0.0)
         nc.scalar.activation(out=warm[:], in_=warm[:], func=ACT.Gelu)
-        nc.vector.memset(w_scales[:].rearrange("p g f -> p (g f)").bitcast(I32), 0)
+        for groups in (slice(0, UNIT_GROUPS), slice(UNIT_GROUPS, K_GROUPS)):
+            nc.vector.memset(w_scales[:, groups, :].rearrange("p g f -> p (g f)").bitcast(I32), 0)
         nc.vector.memset(rows[:], 0.0)
         nc.vector.memset(ones[:], 1.0)
         nc.vector.memset(minus_half[:], -0.5)
@@ -277,9 +280,11 @@ def tile_gcnlayer_pa_k_kernel(tc, x, adj, W1_words, W1_scales, b1, ln_gamma, ln_
             if s < steps:
                 load_step(s)
                 if s == 0:
-                    load_scales()
+                    load_scales(0, UNIT_GROUPS)
                 if 0 < s <= QUARTERS:
                     load_weights(s - 1)
+                if s == 1:
+                    load_scales(UNIT_GROUPS, K_GROUPS)
                 for i, n in adj_of.items():
                     if s == min(turns[i][-1] + 1, steps - 1):
                         load_adj(n)
@@ -312,7 +317,7 @@ def tile_gcnlayer_pa_k_kernel(tc, x, adj, W1_words, W1_scales, b1, ln_gamma, ln_
                 spread(0, bank)
                 nc.scalar.copy(out=b1_spread[:], in_=bank[:, 0:FEAT])
             finished = [n for n in range(TILES) if LAST_STEP[n] in range(turns[i - 1][0], turn[0])] if i else []
-            scale_now = [i - 4] if 0 <= i - 4 < TILES - 1 else []
+            scale_now = [i - 5] if 0 <= i - 5 < TILES - 1 else []
             next_steps = turns[min(i + 1, len(turns) - 1)]
             sort_now = list(range(sorted_to, min(next_steps[-1] + 2, steps)))
             for j in range(2):

@@ -73,14 +73,14 @@ def tile_gcnlayer_pa_k_kernel(tc, x, adj, W1_words, W1_scales, b1, ln_gamma, ln_
         scaled_b1 = keep.tile([P, FEAT], F32)
         minus_half = keep.tile([P, 1], F32)
         warm = keep.tile([P, 1], F32)
-        w_codes = keep.tile([P, K_GROUPS, FEAT], U32, align_bytes=64)
-        w_scales = keep.tile([P, K_GROUPS, FEAT], U8, align_bytes=64)
-        adj_codes = keep.tile([P, TILES, NODE_GROUPS, P], U32, align_bytes=64)
-        adj_scales = keep.tile([P, TILES, NODE_GROUPS, P], U8, align_bytes=64)
+        w_codes = keep.tile([P, K_GROUPS, FEAT], U32, align_bytes=256)
+        w_scales = keep.tile([P, K_GROUPS, 512], U8, align_bytes=256)
+        adj_codes = keep.tile([P, TILES, NODE_GROUPS, P], U32, align_bytes=256)
+        adj_scales = keep.tile([P, TILES, NODE_GROUPS, P], U8, align_bytes=256)
         hb = keep.tile([P, TILES, FEAT], F32)
         hs_grouped = keep.tile([P, NODE_GROUPS, FEAT, PACK], BF16, align_bytes=64)
-        hs_codes = keep.tile([P, NODE_GROUPS, FEAT], U32, align_bytes=64)
-        hs_scales = keep.tile([P, NODE_GROUPS, FEAT], U8, align_bytes=64)
+        hs_codes = keep.tile([P, NODE_GROUPS, FEAT], U32, align_bytes=256)
+        hs_scales = keep.tile([P, NODE_GROUPS, FEAT], U8, align_bytes=256)
         deg = keep.tile([P, TILES], F32)
         dinv = keep.tile([P, TILES], F32)
         g_sum = keep.tile([P, TILES], F32)
@@ -117,7 +117,7 @@ def tile_gcnlayer_pa_k_kernel(tc, x, adj, W1_words, W1_scales, b1, ln_gamma, ln_
         def load_scales(first, last):
             for quadrant in range(4):
                 nc.sync.dma_start(
-                    out=w_scales[32 * quadrant : 32 * quadrant + 4, first:last, :].bitcast(I32),
+                    out=w_scales[32 * quadrant : 32 * quadrant + 4, first:last, 0:FEAT].bitcast(I32),
                     in_=W1_scales[first:last, 4 * quadrant : 4 * quadrant + 4, :]
                     .rearrange("g r f -> r g f")
                     .bitcast(I32),
@@ -167,8 +167,8 @@ def tile_gcnlayer_pa_k_kernel(tc, x, adj, W1_words, W1_scales, b1, ln_gamma, ln_
                 )
 
         def quantise_x(s):
-            x_codes[s] = codes_pool.tile([P, 2, UNIT_COLS], U32, name="x_codes", align_bytes=64)
-            x_scales[s] = codes_pool.tile([P, 2, UNIT_COLS], U8, name="x_scales", align_bytes=64)
+            x_codes[s] = codes_pool.tile([P, 2, UNIT_COLS], U32, name="x_codes", align_bytes=256)
+            x_scales[s] = codes_pool.tile([P, 2, UNIT_COLS], U8, name="x_scales", align_bytes=256)
             for a in range(2):
                 nc.vector.quantize_mx(
                     out=x_codes[s][:, a, :].bitcast(FP8X4), scales=x_scales[s][:, a, :], in_=grouped[s][:, a, :]

from contextlib import ExitStack

import concourse.mybir as mybir
from concourse.masks import make_identity

F32 = mybir.dt.float32
BF16 = mybir.dt.bfloat16
I32 = mybir.dt.int32
U32 = mybir.dt.uint32
U8 = mybir.dt.uint8
FP8X4 = mybir.dt.float8_e4m3fn_x4
ACT = mybir.ActivationFunctionType
ALU = mybir.AluOpType

P = 128
PACK = 4
K_PASS = P * PACK
NODES = 1024
K = 8192
FEAT = 384
EPS = 1e-6

TILES = NODES // P
NODE_GROUPS = NODES // K_PASS
TILES_PER_GROUP = TILES // NODE_GROUPS
K_GROUPS = K // K_PASS
QUARTERS = 4
UNIT_GROUPS = K_GROUPS // QUARTERS
UNIT_K = K // QUARTERS
UNIT_COLS = UNIT_GROUPS * P
BANK_GROUPS = 2
WIDE = 256
FEATURE_CUTS = ((0, WIDE), (WIDE, FEAT))

STEPS = [((0, q), (1, q)) for q in range(QUARTERS)] + [
    ((n, q), (n, q + 1)) for n in range(2, TILES) for q in (0, 2)
]
LAST_STEP = {n: max(s for s, units in enumerate(STEPS) if n in (units[0][0], units[1][0])) for n in range(TILES)}
SINGLE_TURNS = 8
RAW_BUFS = 4

FLOPS = 2 * NODES * K * FEAT + 2 * NODES * NODES * FEAT


def tile_gcnlayer_pa_k_kernel(tc, x, adj, W1_words, W1_scales, b1, ln_gamma, ln_beta, out):
    nc = tc.nc

    def by_node_tile(dram):
        return dram.rearrange("(n p e) w -> n e p w", n=TILES // 2, p=P, e=2)

    x_tiles = by_node_tile(x)
    adj_tiles = by_node_tile(adj)
    out_tiles = by_node_tile(out)

    with ExitStack() as ctx:
        ctx.enter_context(tc.manual_schedule())
        keep = ctx.enter_context(tc.tile_pool(name="keep", bufs=1))
        raw_pool = ctx.enter_context(tc.tile_pool(name="raw", bufs=RAW_BUFS))
        sorted_pool = ctx.enter_context(tc.tile_pool(name="sorted", bufs=4))
        grouped_pool = ctx.enter_context(tc.tile_pool(name="grouped", bufs=3))
        codes_pool = ctx.enter_context(tc.tile_pool(name="codes", bufs=4))
        adj_raw_pool = ctx.enter_context(tc.tile_pool(name="adj_raw", bufs=4))
        adj_pool = ctx.enter_context(tc.tile_pool(name="adj", bufs=2))
        tail_pool = ctx.enter_context(tc.tile_pool(name="tail", bufs=4))
        h_banks = ctx.enter_context(tc.psum_pool(name="h_banks", bufs=2))
        banks = ctx.enter_context(tc.psum_pool(name="banks", bufs=4))
        narrow_banks = ctx.enter_context(tc.psum_pool(name="narrow_banks", bufs=2))

        identity = keep.tile([P, P], F32)
        ones = keep.tile([P, P], BF16)
        rows = keep.tile([P, 3, 512], BF16)
        b1_spread = keep.tile([P, FEAT], F32)
        scaled_b1 = keep.tile([P, FEAT], F32)
        minus_half = keep.tile([P, 1], F32)
        warm = keep.tile([P, 1], F32)
        w_codes = keep.tile([P, K_GROUPS, FEAT], U32, align_bytes=256)
        w_scales = keep.tile([P, K_GROUPS, 512], U8, align_bytes=256)
        adj_codes = keep.tile([P, TILES, NODE_GROUPS, P], U32, align_bytes=256)
        adj_scales = keep.tile([P, TILES, NODE_GROUPS, P], U8, align_bytes=256)
        hb = keep.tile([P, TILES, FEAT], F32)
        hs_grouped = keep.tile([P, NODE_GROUPS, FEAT, PACK], BF16, align_bytes=64)
        hs_codes = keep.tile([P, NODE_GROUPS, FEAT], U32, align_bytes=256)
        hs_scales = keep.tile([P, NODE_GROUPS, FEAT], U8, align_bytes=256)
        deg = keep.tile([P, TILES], F32)
        dinv = keep.tile([P, TILES], F32)
        g_sum = keep.tile([P, TILES], F32)
        minus_mean = keep.tile([P, TILES], F32)
        sq_sum = keep.tile([P, TILES], F32)
        var_eps = keep.tile([P, TILES], F32)
        rstd = keep.tile([P, TILES], F32)

        raw = {}
        ordered = {}
        grouped = {}
        x_codes = {}
        x_scales = {}
        adj_raw = {}
        adj_grouped = {}
        h_acc = {}
        filled = []
        narrow_free = []

        def load_step(s):
            raw[s] = raw_pool.tile([P, 2, UNIT_K], BF16, name="raw")
            (n0, q0), (n1, q1) = STEPS[s]
            if n0 == n1 and s > QUARTERS + 1:
                nc.sync.dma_start(
                    out=raw[s][:].rearrange("n a k -> n (a k)"),
                    in_=x_tiles[n0 // 2, n0 % 2, :, q0 * UNIT_K : (q1 + 1) * UNIT_K],
                )
            else:
                for a, (n, q) in enumerate(STEPS[s]):
                    nc.sync.dma_start(
                        out=raw[s][:, a, :], in_=x_tiles[n // 2, n % 2, :, q * UNIT_K : (q + 1) * UNIT_K]
                    )

        def load_scales(first, last):
            for quadrant in range(4):
                nc.sync.dma_start(
                    out=w_scales[32 * quadrant : 32 * quadrant + 4, first:last, 0:FEAT].bitcast(I32),
                    in_=W1_scales[first:last, 4 * quadrant : 4 * quadrant + 4, :]
                    .rearrange("g r f -> r g f")
                    .bitcast(I32),
                )

        def load_weights(q):
            groups = slice(q * UNIT_GROUPS, (q + 1) * UNIT_GROUPS)
            nc.sync.dma_start(
                out=w_codes[:, groups, :].bitcast(I32),
                in_=W1_words[groups].rearrange("g p f t -> p g (f t)").bitcast(I32),
            )

        def load_adj(n):
            adj_raw[n] = adj_raw_pool.tile([P, NODES], BF16, name="adj_raw")
            nc.sync.dma_start(out=adj_raw[n][:], in_=adj_tiles[n // 2, n % 2, :, :])

        def sort_words(s):
            ordered[s] = sorted_pool.tile([P, 2, UNIT_K], BF16, name="ordered")
            for a in range(2):
                nc.vector.tensor_copy(
                    out=ordered[s][:, a, :].bitcast(F32).rearrange("n (g u p) -> n g p u", g=UNIT_GROUPS, u=2),
                    in_=raw[s][:, a, :].bitcast(F32).rearrange("n (g p u) -> n g p u", g=UNIT_GROUPS, u=2),
                )

        def next_bank():
            turn = len(filled) % 6 if narrow_free else len(filled) % 4
            filled.append(turn)
            if turn < 4:
                bank = banks.tile([P, BANK_GROUPS, 2, P], F32, name="bank")
            else:
                bank = narrow_banks.tile([P, BANK_GROUPS, 2, P], F32, name="narrow")
            return bank

        def transpose_x(s, a):
            if a == 0:
                grouped[s] = grouped_pool.tile([P, 2, UNIT_K], BF16, name="grouped", align_bytes=64)
            words = ordered[s][:, a, :].bitcast(F32).rearrange("n (g u p) -> n g u p", g=UNIT_GROUPS, u=2)
            pairs = grouped[s][:, a, :].bitcast(F32).rearrange("p (g n u) -> p g n u", g=UNIT_GROUPS, u=2)
            for g0 in range(0, UNIT_GROUPS, BANK_GROUPS):
                bank = next_bank()
                for g in range(BANK_GROUPS):
                    for u in range(2):
                        nc.tensor.transpose(bank[:, g, u, :], words[:, g0 + g, u, :], identity[:])
                nc.scalar.copy(
                    out=pairs[:, g0 : g0 + BANK_GROUPS, :, :],
                    in_=bank[:].rearrange("p g u n -> p g n u"),
                )

        def quantise_x(s):
            x_codes[s] = codes_pool.tile([P, 2, UNIT_COLS], U32, name="x_codes", align_bytes=256)
            x_scales[s] = codes_pool.tile([P, 2, UNIT_COLS], U8, name="x_scales", align_bytes=256)
            for a in range(2):
                nc.vector.quantize_mx(
                    out=x_codes[s][:, a, :].bitcast(FP8X4), scales=x_scales[s][:, a, :], in_=grouped[s][:, a, :]
                )

        def first_matmul(s, cut):
            first, last = FEATURE_CUTS[cut]
            for a, (n, q) in enumerate(STEPS[s]):
                if q == 0 and (cut == 0 or n == TILES - 1):
                    h_acc[n, cut] = h_banks.tile([P, 512], F32, name="h_acc")
                elif q == 0 and s == 0:
                    h_acc[n, cut] = narrow_banks.tile([P, 512], F32, name="narrow")
                elif q == 0:
                    h_acc[n, cut] = h_acc[n, 0]
                for g in range(UNIT_GROUPS):
                    k_group = q * UNIT_GROUPS + g
                    nodes = slice(g * P, (g + 1) * P)
                    nc.tensor.matmul_mx(
                        out=h_acc[n, cut][:, first:last],
                        lhsT=x_codes[s][:, a, nodes].bitcast(FP8X4),
                        lhsT_scale=x_scales[s][:, a, nodes],
                        rhs=w_codes[:, k_group, first:last].bitcast(FP8X4),
                        rhs_scale=w_scales[:, k_group, first:last],
                        start=(k_group == 0),
                        stop=(k_group == K_GROUPS - 1),
                    )

        def transpose_adj(n):
            words = adj_raw[n][:].bitcast(F32).rearrange("i (c u p) -> i c u p", c=NODE_GROUPS, u=2)
            bank = next_bank()
            for c in range(NODE_GROUPS):
                for u in range(2):
                    nc.tensor.transpose(bank[:, c, u, :], words[:, c, u, :], identity[:])
            adj_grouped[n] = adj_pool.tile([P, NODES], BF16, name="adj_grouped", align_bytes=64)
            nc.scalar.copy(
                out=adj_grouped[n][:].bitcast(F32).rearrange("p (c i u) -> p c i u", c=NODE_GROUPS, u=2),
                in_=bank[:].rearrange("p c u i -> p c i u"),
            )

        def degree(n):
            unused = adj_pool.tile([P, NODES], BF16, name="unused")
            if n < TILES - 1:
                nc.scalar.activation(
                    out=unused[:], in_=adj_raw[n][:], func=ACT.Copy, bias=1.0 / NODES, accum_out=deg[:, n : n + 1]
                )
            else:
                nc.vector.tensor_scalar(
                    out=unused[:], in0=adj_raw[n][:], scalar1=1.0, scalar2=1.0, op0=ALU.mult, op1=ALU.add,
                    accum_out=deg[:, n : n + 1],
                )
            nc.gpsimd.tensor_tensor(out=dinv[:, n : n + 1], in0=deg[:, n : n + 1], in1=minus_half[:], op=ALU.pow)

        def quantise_adj(n):
            nc.vector.quantize_mx(
                out=adj_codes[:, n, :, :].rearrange("p c i -> p (c i)").bitcast(FP8X4),
                scales=adj_scales[:, n, :, :].rearrange("p c i -> p (c i)"),
                in_=adj_grouped[n][:],
            )

        def add_bias(n):
            split = FEATURE_CUTS if n < 2 or n == TILES - 1 else ((0, FEAT),)
            for cut, (first, last) in enumerate(split):
                nc.vector.tensor_tensor(
                    out=hb[:, n, first:last], in0=h_acc[n, cut][:, first:last], in1=b1_spread[:, first:last],
                    op=ALU.add,
                )

        def scale_h(n, first, last):
            c, t = divmod(n, TILES_PER_GROUP)
            nc.vector.tensor_scalar(
                out=hs_grouped[:, c, first:last, t], in0=hb[:, n, first:last], scalar1=dinv[:, n : n + 1],
                scalar2=None, op0=ALU.mult,
            )

        def last_hs(cut):
            n = TILES - 1
            first, last = FEATURE_CUTS[cut]
            nc.vector.scalar_tensor_tensor(
                out=hs_grouped[:, NODE_GROUPS - 1, first:last, PACK - 1], in0=h_acc[n, cut][:, first:last],
                scalar=dinv[:, n : n + 1], in1=scaled_b1[:, first:last], op0=ALU.mult, op1=ALU.add,
            )

        def quantise_hs(c, first, last):
            nc.vector.quantize_mx(
                out=hs_codes[:, c, first:last].bitcast(FP8X4),
                scales=hs_scales[:, c, first:last],
                in_=hs_grouped[:, c, first:last, :].rearrange("p f t -> p (f t)"),
            )

        nc.vector.memset(warm[:], 0.0)
        nc.scalar.activation(out=warm[:], in_=warm[:], func=ACT.Gelu)
        for groups in (slice(0, UNIT_GROUPS), slice(UNIT_GROUPS, K_GROUPS)):
            nc.vector.memset(w_scales[:, groups, :].rearrange("p g f -> p (g f)").bitcast(I32), 0)
        nc.vector.memset(rows[:], 0.0)
        nc.vector.memset(ones[:], 1.0)
        nc.vector.memset(minus_half[:], -0.5)
        make_identity(nc, identity[:])
        for v, vector in enumerate((b1, ln_gamma, ln_beta)):
            nc.gpsimd.dma_start(out=rows[0:1, v, 0:FEAT], in_=vector.rearrange("(o f) -> o f", o=1))

        def spread(v, tile):
            nc.tensor.matmul(out=tile[:], lhsT=ones[:], rhs=rows[:, v, :], start=True, stop=True)

        steps = len(STEPS)
        turns = [(s,) for s in range(SINGLE_TURNS)] + [(s, s + 1) for s in range(SINGLE_TURNS, steps, 2)]
        adj_of = {len(turns) - TILES + n: n for n in range(TILES)}

        def load_turn(s):
            if s < steps:
                load_step(s)
                if s == 0:
                    load_scales(0, UNIT_GROUPS)
                if 0 < s <= QUARTERS:
                    load_weights(s - 1)
                if s == 1:
                    load_scales(UNIT_GROUPS, K_GROUPS)
                for i, n in adj_of.items():
                    if s == min(turns[i][-1] + 1, steps - 1):
                        load_adj(n)

        for s in range(RAW_BUFS):
            load_turn(s)
        loaded = RAW_BUFS
        for s in range(2):
            sort_words(s)
            load_turn(loaded)
            loaded += 1
            if s == 0:
                for a in range(2):
                    transpose_x(0, a)
        sorted_to = 2
        transposed_to = 1

        for i, turn in enumerate(turns):
            for s in range(transposed_to, min(turn[-1] + 2, steps)):
                for a in range(2):
                    transpose_x(s, a)
            transposed_to = turn[-1] + 2
            if i in adj_of:
                transpose_adj(adj_of[i])
                if adj_of[i] < TILES - 1:
                    degree(adj_of[i])
            if i == 2:
                bank = banks.tile([P, 512], F32, name="bank")
                filled.append(0)
                spread(0, bank)
                nc.scalar.copy(out=b1_spread[:], in_=bank[:, 0:FEAT])
            finished = [n for n in range(TILES) if LAST_STEP[n] in range(turns[i - 1][0], turn[0])] if i else []
            scale_now = [i - 5] if 0 <= i - 5 < TILES - 1 else []
            next_steps = turns[min(i + 1, len(turns) - 1)]
            sort_now = list(range(sorted_to, min(next_steps[-1] + 2, steps)))
            for j in range(2):
                if j < len(turn):
                    quantise_x(turn[j])
                for n in finished if j == 0 else ():
                    add_bias(n)
                    if n == 1:
                        narrow_free.append(True)
                if j == 0 and i + 1 == len(turns):
                    degree(TILES - 1)
                for s in sort_now[j : j + 1]:
                    sort_words(s)
                    sorted_to = s + 1
                    load_turn(loaded)
                    loaded += 1
            if i - 1 in adj_of:
                quantise_adj(adj_of[i - 1])
            if i + 1 == len(turns):
                quantise_adj(TILES - 1)
            for n in scale_now:
                scale_h(n, 0, FEAT)
                if n == TILES_PER_GROUP - 1:
                    for first, last in FEATURE_CUTS:
                        quantise_hs(0, first, last)
            if i + 1 == len(turns):
                n = TILES - 1
                nc.scalar.activation(out=scaled_b1[:], in_=b1_spread[:], func=ACT.Copy, scale=dinv[:, n : n + 1])
            for s in turn:
                first_matmul(s, 0)
                if s < QUARTERS:
                    first_matmul(s, 1)
                if i + 1 == len(turns):
                    first_matmul(s, 1)
            if turn[-1] >= QUARTERS and turn[-1] % 2 == 1 and i + 1 < len(turns):
                first_matmul(turn[-1] - 1, 1)
                first_matmul(turn[-1], 1)
        gamma_spread = narrow_banks.tile([P, 512], F32, name="narrow")
        spread(1, gamma_spread)
        beta_spread = narrow_banks.tile([P, 512], F32, name="narrow")
        spread(2, beta_spread)
        for cut, (first, last) in enumerate(FEATURE_CUTS):
            last_hs(cut)
            quantise_hs(NODE_GROUPS - 1, first, last)
        add_bias(TILES - 1)

        gelu = {}
        centred = {}
        summed = {}
        aggs = {}

        def multiply_adj(i, cut):
            if cut == 0:
                aggs[i] = banks.tile([P, 512], F32, name="bank")
            cols = slice(FEATURE_CUTS[cut][0], FEATURE_CUTS[cut][1])
            for c in range(NODE_GROUPS):
                nc.tensor.matmul_mx(
                    out=aggs[i][:, cols],
                    lhsT=adj_codes[:, i, c, :].bitcast(FP8X4),
                    lhsT_scale=adj_scales[:, i, c, :],
                    rhs=hs_codes[:, c, cols].bitcast(FP8X4),
                    rhs_scale=hs_scales[:, c, cols],
                    start=(c == 0),
                    stop=(c == NODE_GROUPS - 1),
                )

        def add_hs(i):
            summed[i] = tail_pool.tile([P, FEAT], F32, name="summed")
            nc.vector.scalar_tensor_tensor(
                out=summed[i][:], in0=hb[:, i, :], scalar=dinv[:, i : i + 1], in1=aggs[i][:, 0:FEAT],
                op0=ALU.mult, op1=ALU.add,
            )

        def activate(i):
            one = slice(i, i + 1)
            gelu[i] = tail_pool.tile([P, FEAT], F32, name="gelu")
            nc.scalar.activation(
                out=gelu[i][:], in_=summed[i][:], func=ACT.Gelu, scale=dinv[:, one], accum_out=g_sum[:, one]
            )

        def mean(i):
            one = slice(i, i + 1)
            nc.scalar.activation(out=minus_mean[:, one], in_=g_sum[:, one], func=ACT.Copy, scale=-1.0 / FEAT)

        def square(i):
            one = slice(i, i + 1)
            squares = tail_pool.tile([P, FEAT], F32, name="squares", bufs=1)
            nc.scalar.activation(
                out=squares[:], in_=gelu[i][:], func=ACT.Square, bias=minus_mean[:, one], scale=1.0,
                accum_out=sq_sum[:, one],
            )

        def deviation(i):
            one = slice(i, i + 1)
            nc.scalar.activation(out=var_eps[:, one], in_=sq_sum[:, one], func=ACT.Copy, scale=1.0 / FEAT, bias=EPS)
            nc.gpsimd.tensor_tensor(out=rstd[:, one], in0=var_eps[:, one], in1=minus_half[:], op=ALU.pow)

        def centre(i):
            centred[i] = tail_pool.tile([P, FEAT], F32, name="centred")
            nc.vector.scalar_tensor_tensor(
                out=centred[i][:], in0=gelu[i][:], scalar=minus_mean[:, i : i + 1], in1=gamma_spread[:, 0:FEAT],
                op0=ALU.add, op1=ALU.mult,
            )

        def scale_and_store(i):
            result = tail_pool.tile([P, FEAT], F32, name="result", bufs=6)
            nc.vector.scalar_tensor_tensor(
                out=result[:], in0=centred[i][:], scalar=rstd[:, i : i + 1], in1=beta_spread[:, 0:FEAT],
                op0=ALU.mult, op1=ALU.add,
            )
            nc.sync.dma_start(out=out_tiles[i // 2, i % 2, :, :], in_=result[:])

        for cut in range(2):
            for i in range(4):
                multiply_adj(i, cut)
        for i in range(2):
            add_hs(i)
        for step in range(TILES + 2):
            if step + 2 < TILES:
                if step + 2 >= 4:
                    for cut in range(2):
                        multiply_adj(step + 2, cut)
                add_hs(step + 2)
            if step < TILES:
                activate(step)
            if 0 <= step - 1 < TILES:
                square(step - 1)
            if step < TILES:
                mean(step)
            if 0 <= step - 1 < TILES:
                deviation(step - 1)
                centre(step - 1)
            if 0 <= step - 2 < TILES:
                scale_and_store(step - 2)
